import numpy as np
import ml_dtypes


def mxq(x, axis, fmt="e4m3"):
    dtype, down = {"e4m3": (ml_dtypes.float8_e4m3fn, 7), "e5m2": (ml_dtypes.float8_e5m2, 14)}[fmt]
    v = np.moveaxis(np.asarray(x, np.float32).astype(ml_dtypes.bfloat16).astype(np.float64), axis, -1)
    blocks = v.reshape(v.shape[:-1] + (-1, 32))
    amax = np.abs(blocks).max(-1, keepdims=True)
    byte = np.maximum(np.where(amax > 0, np.frexp(amax)[1] - 1 + 127, 0) - down, 1)
    scale = np.exp2(byte - 127.0)
    codes = (blocks / scale).astype(np.float32).astype(dtype).astype(np.float64)
    return np.moveaxis((codes * scale).reshape(v.shape), -1, axis)


WIDE = False


def mx_kscale(k):
    if not WIDE:
        return np.ones(k)
    levels = np.array([10, -10, 5, -5, 0])
    if k % 512:
        return np.exp2(np.random.permutation(np.resize(levels, k // 32))).repeat(32)
    a = np.empty((k // 512, 16))
    for p in range(k // 512):
        a[p, :8] = np.random.permutation(np.resize(levels, 8))
        for g in range(8):
            far = levels[np.abs(levels - a[p, g]) >= 10]
            a[p, g + 8] = far[np.random.randint(len(far))]
    return np.exp2(a.ravel()).repeat(32)


BF16 = ml_dtypes.bfloat16


def bf(x):
    return np.asarray(x, np.float32).astype(BF16)


def f64(x):
    return np.asarray(x).astype(np.float64)


B, STACK, TUBE, CH, IMG, PATCH, EMBED = 4, 16, 2, 1, 96, 16, 1024
GH = IMG // PATCH
GW = IMG // PATCH
GD = STACK // TUBE
K = TUBE * CH * PATCH * PATCH


def _sincos_1d(dim, pos):
    omega = 1.0 / (10000.0 ** (np.arange(dim // 2, dtype=np.float64) / (dim / 2.0)))
    out = pos[:, None].astype(np.float64) * omega[None, :]
    return np.concatenate([np.sin(out), np.cos(out)], axis=1)


def get_3d_sincos_pos_embed(grid_h, grid_w, grid_depth, embed_dim):
    dim_t = embed_dim // 4
    dim_s = embed_dim - dim_t
    emb_t = _sincos_1d(dim_t, np.arange(grid_depth))
    emb_h = _sincos_1d(dim_s // 2, np.arange(grid_h))
    emb_w = _sincos_1d(dim_s - dim_s // 2, np.arange(grid_w))
    emb_hw = np.concatenate([np.repeat(emb_h, grid_w, axis=0), np.tile(emb_w, (grid_h, 1))], axis=1)
    ns = grid_h * grid_w
    return np.concatenate([np.repeat(emb_t, ns, axis=0), np.tile(emb_hw, (grid_depth, 1))], axis=1)


def setup_inputs():
    s = mx_kscale(K)
    sv = s.reshape(TUBE, CH, PATCH, PATCH)[:, :, None, :, None, :]
    video = np.random.standard_normal((B, GD, TUBE, CH, GH, PATCH, GW, PATCH)) * sv
    return {"video": bf(video.reshape(B, STACK, CH, IMG, IMG)),
            "W": bf(np.random.standard_normal((EMBED, K)) / np.sqrt(K) / s[None, :]),
            "b": bf(np.random.standard_normal(EMBED) * 0.3),
            "pos_embed": bf(get_3d_sincos_pos_embed(GH, GW, GD, EMBED)[None])}


def core(video, W, b, pos_embed):
    video = f64(video)
    B_, T, C, H, W_ = video.shape
    p = PATCH
    gh, gw = H // p, W_ // p
    ns = gh * gw
    x = video.reshape(B_ * T, C, gh, p, gw, p)
    x = x.transpose(0, 2, 4, 1, 3, 5)
    x = x.reshape(B_, T, ns, C * p * p)
    x = x.reshape(B_, GD, TUBE, ns, C * p * p)
    x = x.transpose(0, 1, 3, 2, 4)
    tubelets = x.reshape(B_, GD * ns, TUBE * C * p * p)
    tokens = (mxq(tubelets, 2, "e4m3") @ mxq(f64(W), 1, "e4m3").T) + f64(b) + f64(pos_embed)
    return tokens


def e4m3fn_bytes(y):
    return np.clip(np.asarray(y, np.float64), -448.0, 448.0).astype(np.float32).astype(ml_dtypes.float8_e4m3fn).view(np.uint8)


Y_SCALE = 170.0


def reference(video, W, b, pos_embed):
    out = core(video, W, b, pos_embed)
    return out, e4m3fn_bytes(out * Y_SCALE)

@@ -1,0 +1,295 @@
+from contextlib import ExitStack
+
+import concourse.mybir as mybir
+from concourse.masks import make_identity
+
+F32 = mybir.dt.float32
+BF16 = mybir.dt.bfloat16
+U32 = mybir.dt.uint32
+U8 = mybir.dt.uint8
+FP8X4 = mybir.dt.float8_e4m3fn_x4
+FP8 = mybir.dt.float8_e4m3fn
+ACT = mybir.ActivationFunctionType
+ALU = mybir.AluOpType
+
+P = 128
+EMBED = 1024
+NH = 512
+Y_SCALE = 170.0
+FLOPS = 2 * 1152 * 512 * 1024
+
+
+def tile_tubeletembedding_kernel(tc, video, W, b, pos_embed, out_0, out_1):
+    nc = tc.nc
+
+    vid = video[:, :, 0, :, :].rearrange(
+        "b (d ts) (ih il py) x -> ts il (b d) ih (py x)", ts=2, ih=2, il=3
+    )
+    wv = W.rearrange("(eb p) k -> p eb k", p=P)
+    pv = pos_embed[0].rearrange("(a q) e -> a q e", q=18)
+    o0_bh = out_0.rearrange("b (a q) e -> b a q e", q=18)
+    o1_bh = out_1.rearrange("b (a q) e -> b a q e", q=18)
+    o0_9 = out_0.rearrange("b (a q) e -> (b a) q e", q=18)
+    o1_9 = out_1.rearrange("b (a q) e -> (b a) q e", q=18)
+
+    with ExitStack() as ctx:
+        keep = ctx.enter_context(tc.tile_pool(name="keep", bufs=1))
+        outp = ctx.enter_context(tc.tile_pool(name="outp", bufs=9))
+        tps = ctx.enter_context(tc.psum_pool(name="tps", bufs=4))
+        accs = ctx.enter_context(tc.psum_pool(name="accs", bufs=4))
+
+        ident = keep.tile([P, P], F32, name="ident")
+        ones = keep.tile([P, P], BF16, name="ones")
+        brow = keep.tile([P, EMBED], BF16, name="brow")
+        bb_sb = keep.tile([P, EMBED], BF16, name="bb_sb")
+        scr = keep.tile([P, 2], F32, name="scr")
+        warm = keep.tile([P, NH], BF16, name="warm")
+        x_raw = [keep.tile([P, 2, 1536], BF16, name="x_raw%d" % t) for t in range(2)]
+        w_raw = [keep.tile([P, 2, 512], BF16, name="w_raw%d" % c) for c in range(4)]
+        pos_t = [keep.tile([P, EMBED], BF16, name="pos_t%d" % s) for s in range(3)]
+        posb = [keep.tile([P, EMBED], F32, name="posb%d" % s) for s in range(3)]
+        y0 = [keep.tile([P, 2, 2, P], F32, name="y0_%d" % jp) for jp in range(3)]
+        y1 = [keep.tile([P, 2, 32, 16], BF16, name="y1_%d" % jp) for jp in range(3)]
+        w_g = [keep.tile([P, 4 * NH], BF16, name="w_g%d" % h, align_bytes=64) for h in range(2)]
+        w_c = [keep.tile([P, NH], U32, name="w_c%d" % h, align_bytes=64) for h in range(2)]
+        w_s = [keep.tile([P, NH], U8, name="w_s%d" % h, align_bytes=64) for h in range(2)]
+        a_cols = [512, 512, 128]
+        a_g = [keep.tile([P, 4 * a_cols[s]], BF16, name="a_g%d" % s, align_bytes=64) for s in range(3)]
+        a_c = [keep.tile([P, a_cols[s]], U32, name="a_c%d" % s, align_bytes=64) for s in range(3)]
+        a_s = [keep.tile([P, a_cols[s]], U8, name="a_s%d" % s, align_bytes=64) for s in range(3)]
+
+        wt = {}
+        xt = {}
+        bbp = {}
+        acc = {}
+        o32 = {}
+        o8 = {}
+
+        def copy_on(eng, out, in_):
+            if eng == "S":
+                nc.scalar.copy(out=out, in_=in_)
+            else:
+                nc.vector.tensor_copy(out=out, in_=in_)
+
+        def w_T(c):
+            ww = w_raw[c][:].bitcast(F32)
+            wt[c] = tps.tile([P, 2, 2, P], F32, name="wt", tag="tp")
+            for ebl in range(2):
+                for u in range(2):
+                    nc.tensor.transpose(wt[c][:, ebl, u, :], ww[:, ebl, u::2], ident[:])
+
+        def w_copy(c, eng):
+            dst = w_g[c // 2][:].bitcast(F32)[:, 512 * (c % 2) : 512 * (c % 2) + 512].rearrange(
+                "p (eb e u) -> p eb e u", eb=2, u=2
+            )
+            copy_on(eng, dst, wt[c][:].rearrange("p eb u e -> p eb e u"))
+
+        def w_quant(c):
+            h, c2 = c // 2, c % 2
+            nc.vector.quantize_mx(
+                out=w_c[h][:, 256 * c2 : 256 * c2 + 256].bitcast(FP8X4),
+                scales=w_s[h][:, 256 * c2 : 256 * c2 + 256],
+                in_=w_g[h][:, 1024 * c2 : 1024 * c2 + 1024],
+            )
+
+        def bb_mm(nh):
+            bbp[nh] = accs.tile([P, NH], F32, name="bbp", tag="acc")
+            nc.tensor.matmul(bbp[nh][:], lhsT=ones[:], rhs=brow[:, NH * nh : NH * nh + NH], start=True, stop=True)
+
+        def bb_copy(nh, eng):
+            copy_on(eng, bb_sb[:, NH * nh : NH * nh + NH], bbp[nh][:])
+
+        def x_relay(t, jp, eng="G"):
+            if t == 0:
+                xw = x_raw[0][:].bitcast(F32).rearrange(
+                    "p ts (py j wq u) -> p j u (ts py) wq", py=16, j=6, wq=4, u=2
+                )
+                copy_on(
+                    eng,
+                    y0[jp][:].rearrange("p jj u (tp wq) -> p jj u tp wq", wq=4),
+                    xw[:, 2 * jp : 2 * jp + 2],
+                )
+            else:
+                xb = x_raw[1][:].rearrange("p ts (py j px) -> p j (ts py) px", py=16, j=6, px=16)
+                nc.gpsimd.tensor_scalar(
+                    out=y1[jp][:], in0=xb[:, 2 * jp : 2 * jp + 2], scalar1=1.0, scalar2=0.0,
+                    op0=ALU.mult, op1=ALU.add,
+                )
+
+        def x_T(t, jp):
+            xt[(t, jp)] = tps.tile([P, 2, 2, P], F32, name="xt", tag="tp")
+            for jj in range(2):
+                for u in range(2):
+                    if t == 0:
+                        src = y0[jp][:, jj, u, :]
+                    else:
+                        src = y1[jp][:].rearrange("p jj tp px -> p jj (tp px)").bitcast(F32)[:, jj, u::2]
+                    nc.tensor.transpose(xt[(t, jp)][:, jj, u, :], src, ident[:])
+
+        def x_copy(t, jp, il2, eng):
+            il = il2 if t == 0 else 2
+            q = 6 * il + 2 * jp
+            s, qq, nq = (q // 8, q % 8, 8) if q < 16 else (2, q - 16, 2)
+            dst = a_g[s][:].bitcast(F32).rearrange("p (a q u) -> p a q u", q=nq, u=2)
+            xv = xt[(t, jp)][:].rearrange("p jj u (a il) -> p il a jj u", il=2)
+            copy_on(eng, dst[:, :, qq : qq + 2, :], xv[:, il2])
+
+        def make_posb(s, nh, eng):
+            sl = slice(NH * nh, NH * nh + NH)
+            if eng == "G":
+                nc.gpsimd.tensor_tensor(out=posb[s][:, sl], in0=pos_t[s][:, sl], in1=bb_sb[:, sl], op=ALU.add)
+            else:
+                nc.vector.tensor_tensor(out=posb[s][:, sl], in0=pos_t[s][:, sl], in1=bb_sb[:, sl], op=ALU.add)
+
+        def a_quant(s, bi):
+            nc.vector.quantize_mx(
+                out=a_c[s][:, P * bi : P * bi + P].bitcast(FP8X4),
+                scales=a_s[s][:, P * bi : P * bi + P],
+                in_=a_g[s][:, 4 * P * bi : 4 * P * bi + 4 * P],
+            )
+
+        def mm(s, bi, nh):
+            acc[(s, bi, nh)] = accs.tile([P, NH], F32, name="acc", tag="acc")
+            nc.tensor.matmul_mx(
+                out=acc[(s, bi, nh)][:],
+                lhsT=a_c[s][:, P * bi : P * bi + P].bitcast(FP8X4),
+                lhsT_scale=a_s[s][:, P * bi : P * bi + P],
+                rhs=w_c[nh][:].bitcast(FP8X4),
+                rhs_scale=w_s[nh][:],
+                start=True,
+                stop=True,
+            )
+
+        def add(s, bi, nh):
+            if (s, bi) not in o32:
+                o32[(s, bi)] = outp.tile([P, EMBED], F32, name="o32", tag="o32")
+                o8[(s, bi)] = outp.tile([P, EMBED], FP8, name="o8", tag="o8")
+            sl = slice(NH * nh, NH * nh + NH)
+            nc.vector.tensor_tensor(out=o32[(s, bi)][:, sl], in0=acc[(s, bi, nh)][:], in1=posb[s][:, sl], op=ALU.add)
+
+        def cast(s, bi, nh):
+            sl = slice(NH * nh, NH * nh + NH)
+            nc.scalar.activation(
+                out=o8[(s, bi)][:, sl], in_=o32[(s, bi)][:, sl], func=ACT.Copy, scale=Y_SCALE, saturate=False
+            )
+
+        def st32(s, bi, lo, hi):
+            d0 = o0_bh[bi, :, 8 * s : 8 * s + 8, lo:hi] if s < 2 else o0_9[:, 16:18, lo:hi]
+            nc.sync.dma_start(out=d0, in_=o32[(s, bi)][:, lo:hi])
+
+        def st8(s, bi):
+            d1 = o1_bh[bi, :, 8 * s : 8 * s + 8, :] if s < 2 else o1_9[:, 16:18, :]
+            nc.sync.dma_start(out=d1, in_=o8[(s, bi)][:].bitcast(U8))
+
+        def dummy():
+            nc.tensor.matmul(junk[:], lhsT=ones[:], rhs=warm[:], start=True, stop=True)
+
+        nc.gpsimd.memset(ones[:], 1.0)
+        nc.gpsimd.memset(warm[:].bitcast(F32), 0.0)
+        nc.gpsimd.memset(scr[:], 0.0)
+        make_identity(nc, ident[:])
+        nc.vector.memset(brow[:].bitcast(F32), 0.0)
+        nc.vector.memset(x_raw[1][:].bitcast(F32), 0.0)
+
+        ctx.enter_context(tc.manual_schedule())
+        nc.scalar.activation(out=scr[:, 1:2], in_=scr[:, 0:1], func=ACT.Copy, scale=1.0)
+
+        for c in range(2):
+            nc.sync.dma_start(out=w_raw[c][:], in_=wv[:, 2 * c : 2 * c + 2, :])
+        nc.sync.dma_start(out=brow[0:1, :], in_=b.rearrange("(o e) -> o e", o=1))
+        for ts in range(2):
+            for il in range(2):
+                nc.sync.dma_start(out=x_raw[0][il::2, ts, :], in_=vid[ts, il])
+        nc.sync.dma_start(out=pos_t[0][:], in_=pv[:, 0:8, :])
+        for c in range(2, 4):
+            nc.sync.dma_start(out=w_raw[c][:], in_=wv[:, 2 * c : 2 * c + 2, :])
+        for ts in range(2):
+            nc.sync.dma_start(out=x_raw[1][0::2, ts, :], in_=vid[ts, 2])
+        nc.sync.dma_start(out=pos_t[1][:], in_=pv[:, 8:16, :])
+        for bi in range(4):
+            nc.sync.dma_start(out=pos_t[2][32 * bi : 32 * bi + 32, :], in_=pv[:, 16:18, :])
+
+        junk = accs.tile([P, NH], F32, name="junk", tag="acc")
+        dummy()
+        dummy()
+        dummy()
+        w_T(0)
+        w_T(1)
+        w_copy(0, "S")
+        bb_mm(0)
+        bb_mm(1)
+        w_copy(1, "S")
+        bb_copy(0, "V")
+        dummy()
+        bb_copy(1, "S")
+        x_relay(0, 0, "V")
+        x_relay(0, 2, "V")
+        x_relay(0, 1, "S")
+        x_T(0, 0)
+        x_T(0, 2)
+        x_T(0, 1)
+        make_posb(0, 0, "G")
+        make_posb(0, 1, "G")
+        w_quant(0)
+        w_quant(1)
+        x_copy(0, 0, 0, "S")
+        x_copy(0, 0, 1, "S")
+        x_copy(0, 2, 0, "V")
+        w_T(2)
+        w_T(3)
+        x_copy(0, 1, 0, "S")
+        for bi in range(4):
+            a_quant(0, bi)
+        x_copy(0, 1, 1, "S")
+        x_copy(0, 2, 1, "S")
+        w_copy(2, "S")
+        w_copy(3, "S")
+        x_relay(1, 0)
+        x_relay(1, 1)
+        make_posb(1, 0, "G")
+        make_posb(1, 1, "G")
+        x_relay(1, 2)
+        make_posb(2, 0, "G")
+        make_posb(2, 1, "G")
+
+        banks = [(0, bi, nh) for nh in range(2) for bi in range(4)]
+        banks += [(1, bi, nh) for bi in range(4) for nh in range(2)]
+        banks += [(2, 0, 0), (2, 0, 1)]
+
+        def mms(lo, hi):
+            for k in range(lo, hi):
+                mm(banks[k][0], banks[k][1], banks[k][2])
+
+        mms(0, 4)
+        for i, (s, bi, nh) in enumerate(banks):
+            add(s, bi, nh)
+            if s != 1:
+                st32(s, bi, NH * nh, NH * nh + NH)
+            elif nh == 1:
+                st32(s, bi, 0, EMBED)
+            if i == 0:
+                w_quant(2)
+                w_quant(3)
+            if i < 4:
+                mms(i + 4, i + 5)
+            if i == 3:
+                x_T(1, 0)
+                x_T(1, 1)
+            if i == 4:
+                x_copy(1, 0, 0, "S")
+            if i == 5:
+                x_copy(1, 1, 0, "S")
+            if i in (6, 7, 9, 11):
+                b2 = (6, 7, 9, 11).index(i)
+                a_quant(1, b2)
+                mms(8 + 2 * b2, 10 + 2 * b2)
+            if i == 11:
+                x_T(1, 2)
+            if i == 13:
+                x_copy(1, 2, 0, "S")
+            if i == 14:
+                a_quant(2, 0)
+                mms(16, 18)
+            cast(s, bi, nh)
+            if nh == 1:
+                st8(s, bi)

@@ -25,7 +25,7 @@ def tile_tubeletembedding_kernel(tc, video, W, b, pos_embed, out_0, out_1):
     vid = video[:, :, 0, :, :].rearrange(
         "b (d ts) (ih il py) x -> ts il (b d) ih (py x)", ts=2, ih=2, il=3
     )
-    wv = W.rearrange("(eb p) k -> p eb k", p=P)
+    wv = W.rearrange("(h p e4) k -> h p (e4 k)", p=P, e4=4)
     pv = pos_embed[0].rearrange("(a q) e -> a q e", q=18)
     o0_bh = out_0.rearrange("b (a q) e -> b a q e", q=18)
     o1_bh = out_1.rearrange("b (a q) e -> b a q e", q=18)
@@ -43,13 +43,12 @@ def tile_tubeletembedding_kernel(tc, video, W, b, pos_embed, out_0, out_1):
         brow = keep.tile([P, EMBED], BF16, name="brow")
         bb_sb = keep.tile([P, EMBED], BF16, name="bb_sb")
         scr = keep.tile([P, 2], F32, name="scr")
-        warm = keep.tile([P, NH], BF16, name="warm")
+        wz = keep.tile([P, P], F32, name="wz")
         x_raw = [keep.tile([P, 2, 1536], BF16, name="x_raw%d" % t) for t in range(2)]
-        w_raw = [keep.tile([P, 2, 512], BF16, name="w_raw%d" % c) for c in range(4)]
+        w_raw = [keep.tile([P, 4, 512], BF16, name="w_raw%d" % h) for h in range(2)]
         pos_t = [keep.tile([P, EMBED], BF16, name="pos_t%d" % s) for s in range(3)]
         posb = [keep.tile([P, EMBED], F32, name="posb%d" % s) for s in range(3)]
-        y0 = [keep.tile([P, 2, 2, P], F32, name="y0_%d" % jp) for jp in range(3)]
-        y1 = [keep.tile([P, 2, 32, 16], BF16, name="y1_%d" % jp) for jp in range(3)]
+        y_t = [[keep.tile([P, 2, 2, P], F32, name="y%d_%d" % (t, jp)) for jp in range(3)] for t in range(2)]
         w_g = [keep.tile([P, 4 * NH], BF16, name="w_g%d" % h, align_bytes=64) for h in range(2)]
         w_c = [keep.tile([P, NH], U32, name="w_c%d" % h, align_bytes=64) for h in range(2)]
         w_s = [keep.tile([P, NH], U8, name="w_s%d" % h, align_bytes=64) for h in range(2)]
@@ -71,26 +70,19 @@ def tile_tubeletembedding_kernel(tc, video, W, b, pos_embed, out_0, out_1):
             else:
                 nc.vector.tensor_copy(out=out, in_=in_)
 
-        def w_T(c):
-            ww = w_raw[c][:].bitcast(F32)
-            wt[c] = tps.tile([P, 2, 2, P], F32, name="wt", tag="tp")
-            for ebl in range(2):
+        def w_T(h, g):
+            ww = w_raw[h][:].bitcast(F32)
+            wt[(h, g)] = tps.tile([P, 2, 2, P], F32, name="wt", tag="tp")
+            for e2 in range(2):
                 for u in range(2):
-                    nc.tensor.transpose(wt[c][:, ebl, u, :], ww[:, ebl, u::2], ident[:])
+                    nc.tensor.transpose(wt[(h, g)][:, e2, u, :], ww[:, 2 * g + e2, u::2], ident[:])
 
-        def w_copy(c, eng):
-            dst = w_g[c // 2][:].bitcast(F32)[:, 512 * (c % 2) : 512 * (c % 2) + 512].rearrange(
-                "p (eb e u) -> p eb e u", eb=2, u=2
-            )
-            copy_on(eng, dst, wt[c][:].rearrange("p eb u e -> p eb e u"))
+        def w_copy(h, g, eng):
+            dst = w_g[h][:].bitcast(F32).rearrange("k (p e4 u) -> k p e4 u", e4=4, u=2)
+            copy_on(eng, dst[:, :, 2 * g : 2 * g + 2, :], wt[(h, g)][:].rearrange("k e2 u p -> k p e2 u"))
 
-        def w_quant(c):
-            h, c2 = c // 2, c % 2
-            nc.vector.quantize_mx(
-                out=w_c[h][:, 256 * c2 : 256 * c2 + 256].bitcast(FP8X4),
-                scales=w_s[h][:, 256 * c2 : 256 * c2 + 256],
-                in_=w_g[h][:, 1024 * c2 : 1024 * c2 + 1024],
-            )
+        def w_quant(h):
+            nc.vector.quantize_mx(out=w_c[h][:].bitcast(FP8X4), scales=w_s[h][:], in_=w_g[h][:])
 
         def bb_mm(nh):
             bbp[nh] = accs.tile([P, NH], F32, name="bbp", tag="acc")
@@ -99,32 +91,21 @@ def tile_tubeletembedding_kernel(tc, video, W, b, pos_embed, out_0, out_1):
         def bb_copy(nh, eng):
             copy_on(eng, bb_sb[:, NH * nh : NH * nh + NH], bbp[nh][:])
 
-        def x_relay(t, jp, eng="G"):
-            if t == 0:
-                xw = x_raw[0][:].bitcast(F32).rearrange(
-                    "p ts (py j wq u) -> p j u (ts py) wq", py=16, j=6, wq=4, u=2
-                )
-                copy_on(
-                    eng,
-                    y0[jp][:].rearrange("p jj u (tp wq) -> p jj u tp wq", wq=4),
-                    xw[:, 2 * jp : 2 * jp + 2],
-                )
-            else:
-                xb = x_raw[1][:].rearrange("p ts (py j px) -> p j (ts py) px", py=16, j=6, px=16)
-                nc.gpsimd.tensor_scalar(
-                    out=y1[jp][:], in0=xb[:, 2 * jp : 2 * jp + 2], scalar1=1.0, scalar2=0.0,
-                    op0=ALU.mult, op1=ALU.add,
-                )
+        def x_relay(t, jp, eng):
+            xw = x_raw[t][:].bitcast(F32).rearrange(
+                "p ts (py j wq u) -> p j u (ts py) wq", py=16, j=6, wq=4, u=2
+            )
+            copy_on(
+                eng,
+                y_t[t][jp][:].rearrange("p jj u (tp wq) -> p jj u tp wq", wq=4),
+                xw[:, 2 * jp : 2 * jp + 2],
+            )
 
         def x_T(t, jp):
             xt[(t, jp)] = tps.tile([P, 2, 2, P], F32, name="xt", tag="tp")
             for jj in range(2):
                 for u in range(2):
-                    if t == 0:
-                        src = y0[jp][:, jj, u, :]
-                    else:
-                        src = y1[jp][:].rearrange("p jj tp px -> p jj (tp px)").bitcast(F32)[:, jj, u::2]
-                    nc.tensor.transpose(xt[(t, jp)][:, jj, u, :], src, ident[:])
+                    nc.tensor.transpose(xt[(t, jp)][:, jj, u, :], y_t[t][jp][:, jj, u, :], ident[:])
 
         def x_copy(t, jp, il2, eng):
             il = il2 if t == 0 else 2
@@ -134,12 +115,9 @@ def tile_tubeletembedding_kernel(tc, video, W, b, pos_embed, out_0, out_1):
             xv = xt[(t, jp)][:].rearrange("p jj u (a il) -> p il a jj u", il=2)
             copy_on(eng, dst[:, :, qq : qq + 2, :], xv[:, il2])
 
-        def make_posb(s, nh, eng):
+        def make_posb(s, nh):
             sl = slice(NH * nh, NH * nh + NH)
-            if eng == "G":
-                nc.gpsimd.tensor_tensor(out=posb[s][:, sl], in0=pos_t[s][:, sl], in1=bb_sb[:, sl], op=ALU.add)
-            else:
-                nc.vector.tensor_tensor(out=posb[s][:, sl], in0=pos_t[s][:, sl], in1=bb_sb[:, sl], op=ALU.add)
+            nc.vector.tensor_tensor(out=posb[s][:, sl], in0=pos_t[s][:, sl], in1=bb_sb[:, sl], op=ALU.add)
 
         def a_quant(s, bi):
             nc.vector.quantize_mx(
@@ -181,28 +159,27 @@ def tile_tubeletembedding_kernel(tc, video, W, b, pos_embed, out_0, out_1):
             d1 = o1_bh[bi, :, 8 * s : 8 * s + 8, :] if s < 2 else o1_9[:, 16:18, :]
             nc.sync.dma_start(out=d1, in_=o8[(s, bi)][:].bitcast(U8))
 
-        def dummy():
-            nc.tensor.matmul(junk[:], lhsT=ones[:], rhs=warm[:], start=True, stop=True)
+        def dummy(n):
+            for k in range(n):
+                nc.tensor.matmul(junk[:, 0:P], lhsT=wz[:], rhs=wz[:], start=True, stop=True)
 
-        nc.gpsimd.memset(ones[:], 1.0)
-        nc.gpsimd.memset(warm[:].bitcast(F32), 0.0)
-        nc.gpsimd.memset(scr[:], 0.0)
         make_identity(nc, ident[:])
+        nc.gpsimd.memset(ones[:], 1.0)
+        nc.gpsimd.memset(scr[:], 0.0)
+        nc.vector.memset(wz[:], 0.0)
         nc.vector.memset(brow[:].bitcast(F32), 0.0)
         nc.vector.memset(x_raw[1][:].bitcast(F32), 0.0)
 
         ctx.enter_context(tc.manual_schedule())
         nc.scalar.activation(out=scr[:, 1:2], in_=scr[:, 0:1], func=ACT.Copy, scale=1.0)
 
-        for c in range(2):
-            nc.sync.dma_start(out=w_raw[c][:], in_=wv[:, 2 * c : 2 * c + 2, :])
+        nc.sync.dma_start(out=w_raw[0][:].rearrange("p e k -> p (e k)"), in_=wv[0])
         nc.sync.dma_start(out=brow[0:1, :], in_=b.rearrange("(o e) -> o e", o=1))
         for ts in range(2):
             for il in range(2):
                 nc.sync.dma_start(out=x_raw[0][il::2, ts, :], in_=vid[ts, il])
         nc.sync.dma_start(out=pos_t[0][:], in_=pv[:, 0:8, :])
-        for c in range(2, 4):
-            nc.sync.dma_start(out=w_raw[c][:], in_=wv[:, 2 * c : 2 * c + 2, :])
+        nc.sync.dma_start(out=w_raw[1][:].rearrange("p e k -> p (e k)"), in_=wv[1])
         for ts in range(2):
             nc.sync.dma_start(out=x_raw[1][0::2, ts, :], in_=vid[ts, 2])
         nc.sync.dma_start(out=pos_t[1][:], in_=pv[:, 8:16, :])
@@ -210,47 +187,38 @@ def tile_tubeletembedding_kernel(tc, video, W, b, pos_embed, out_0, out_1):
             nc.sync.dma_start(out=pos_t[2][32 * bi : 32 * bi + 32, :], in_=pv[:, 16:18, :])
 
         junk = accs.tile([P, NH], F32, name="junk", tag="acc")
-        dummy()
-        dummy()
-        dummy()
-        w_T(0)
-        w_T(1)
-        w_copy(0, "S")
+        dummy(4)
         bb_mm(0)
         bb_mm(1)
-        w_copy(1, "S")
         bb_copy(0, "V")
-        dummy()
         bb_copy(1, "S")
-        x_relay(0, 0, "V")
-        x_relay(0, 2, "V")
-        x_relay(0, 1, "S")
+        w_T(0, 0)
+        w_T(0, 1)
+        w_copy(0, 0, "S")
+        w_copy(0, 1, "S")
+        dummy(1)
+        for jp in range(3):
+            x_relay(0, jp, "V")
         x_T(0, 0)
-        x_T(0, 2)
         x_T(0, 1)
-        make_posb(0, 0, "G")
-        make_posb(0, 1, "G")
+        dummy(1)
+        x_T(0, 2)
         w_quant(0)
-        w_quant(1)
+        make_posb(0, 0)
         x_copy(0, 0, 0, "S")
         x_copy(0, 0, 1, "S")
-        x_copy(0, 2, 0, "V")
-        w_T(2)
-        w_T(3)
         x_copy(0, 1, 0, "S")
+        make_posb(0, 1)
+        x_copy(0, 2, 0, "S")
+        w_T(1, 0)
+        dummy(1)
+        w_T(1, 1)
         for bi in range(4):
             a_quant(0, bi)
+        w_copy(1, 0, "S")
+        w_copy(1, 1, "S")
         x_copy(0, 1, 1, "S")
         x_copy(0, 2, 1, "S")
-        w_copy(2, "S")
-        w_copy(3, "S")
-        x_relay(1, 0)
-        x_relay(1, 1)
-        make_posb(1, 0, "G")
-        make_posb(1, 1, "G")
-        x_relay(1, 2)
-        make_posb(2, 0, "G")
-        make_posb(2, 1, "G")
 
         banks = [(0, bi, nh) for nh in range(2) for bi in range(4)]
         banks += [(1, bi, nh) for bi in range(4) for nh in range(2)]
@@ -268,10 +236,12 @@ def tile_tubeletembedding_kernel(tc, video, W, b, pos_embed, out_0, out_1):
             elif nh == 1:
                 st32(s, bi, 0, EMBED)
             if i == 0:
-                w_quant(2)
-                w_quant(3)
+                w_quant(1)
             if i < 4:
                 mms(i + 4, i + 5)
+            if i == 1:
+                x_relay(1, 0, "V")
+                x_relay(1, 1, "S")
             if i == 3:
                 x_T(1, 0)
                 x_T(1, 1)
@@ -279,13 +249,21 @@ def tile_tubeletembedding_kernel(tc, video, W, b, pos_embed, out_0, out_1):
                 x_copy(1, 0, 0, "S")
             if i == 5:
                 x_copy(1, 1, 0, "S")
+                make_posb(1, 0)
+            if i == 6:
+                make_posb(1, 1)
             if i in (6, 7, 9, 11):
                 b2 = (6, 7, 9, 11).index(i)
                 a_quant(1, b2)
                 mms(8 + 2 * b2, 10 + 2 * b2)
+            if i == 8:
+                x_relay(1, 2, "S")
             if i == 11:
                 x_T(1, 2)
+            if i == 12:
+                make_posb(2, 0)
             if i == 13:
+                make_posb(2, 1)
                 x_copy(1, 2, 0, "S")
             if i == 14:
                 a_quant(2, 0)

@@ -44,6 +44,7 @@ def tile_tubeletembedding_kernel(tc, video, W, b, pos_embed, out_0, out_1):
         bb_sb = keep.tile([P, EMBED], BF16, name="bb_sb")
         scr = keep.tile([P, 2], F32, name="scr")
         wz = keep.tile([P, P], F32, name="wz")
+        gs = keep.tile([P, 4], U32, name="gs")
         x_raw = [keep.tile([P, 2, 1536], BF16, name="x_raw%d" % t) for t in range(2)]
         w_raw = [keep.tile([P, 4, 512], BF16, name="w_raw%d" % h) for h in range(2)]
         pos_t = [keep.tile([P, EMBED], BF16, name="pos_t%d" % s) for s in range(3)]
@@ -115,9 +116,18 @@ def tile_tubeletembedding_kernel(tc, video, W, b, pos_embed, out_0, out_1):
             xv = xt[(t, jp)][:].rearrange("p jj u (a il) -> p il a jj u", il=2)
             copy_on(eng, dst[:, :, qq : qq + 2, :], xv[:, il2])
 
-        def make_posb(s, nh):
+        def make_posb(s, nh, eng):
             sl = slice(NH * nh, NH * nh + NH)
-            nc.vector.tensor_tensor(out=posb[s][:, sl], in0=pos_t[s][:, sl], in1=bb_sb[:, sl], op=ALU.add)
+            if eng == "G":
+                nc.gpsimd.tensor_tensor(out=posb[s][:, sl], in0=pos_t[s][:, sl], in1=bb_sb[:, sl], op=ALU.add)
+            else:
+                nc.vector.tensor_tensor(out=posb[s][:, sl], in0=pos_t[s][:, sl], in1=bb_sb[:, sl], op=ALU.add)
+
+        def a_quant_all(s):
+            nc.vector.quantize_mx(out=a_c[s][:].bitcast(FP8X4), scales=a_s[s][:], in_=a_g[s][:])
+
+        def g_sync(k, words):
+            nc.gpsimd.tensor_copy(out=gs[:, k : k + 1], in_=words)
 
         def a_quant(s, bi):
             nc.vector.quantize_mx(
@@ -149,6 +159,13 @@ def tile_tubeletembedding_kernel(tc, video, W, b, pos_embed, out_0, out_1):
             sl = slice(NH * nh, NH * nh + NH)
             nc.scalar.activation(
                 out=o8[(s, bi)][:, sl], in_=o32[(s, bi)][:, sl], func=ACT.Copy, scale=Y_SCALE, saturate=False
+            )
+
+        def cast_v(s, bi, nh):
+            sl = slice(NH * nh, NH * nh + NH)
+            nc.vector.tensor_scalar(
+                out=o8[(s, bi)][:, sl], in0=o32[(s, bi)][:, sl], scalar1=Y_SCALE, scalar2=None, op0=ALU.mult,
+                saturate=False,
             )
 
         def st32(s, bi, lo, hi):
@@ -190,7 +207,7 @@ def tile_tubeletembedding_kernel(tc, video, W, b, pos_embed, out_0, out_1):
         dummy(4)
         bb_mm(0)
         bb_mm(1)
-        bb_copy(0, "V")
+        bb_copy(0, "S")
         bb_copy(1, "S")
         w_T(0, 0)
         w_T(0, 1)
@@ -199,22 +216,24 @@ def tile_tubeletembedding_kernel(tc, video, W, b, pos_embed, out_0, out_1):
         dummy(1)
         for jp in range(3):
             x_relay(0, jp, "V")
-        x_T(0, 0)
-        x_T(0, 1)
-        dummy(1)
-        x_T(0, 2)
+        for jp in range(3):
+            x_T(0, jp)
+        make_posb(0, 0, "V")
         w_quant(0)
-        make_posb(0, 0)
         x_copy(0, 0, 0, "S")
         x_copy(0, 0, 1, "S")
         x_copy(0, 1, 0, "S")
-        make_posb(0, 1)
-        x_copy(0, 2, 0, "S")
+        x_copy(0, 2, 0, "V")
         w_T(1, 0)
         dummy(1)
         w_T(1, 1)
+        dummy(1)
         for bi in range(4):
             a_quant(0, bi)
+        x_relay(1, 0, "V")
+        x_relay(1, 1, "V")
+        g_sync(0, y_t[1][1][:, 0, 0, 0:1].bitcast(U32))
+        make_posb(1, 0, "G")
         w_copy(1, 0, "S")
         w_copy(1, 1, "S")
         x_copy(0, 1, 1, "S")
@@ -229,45 +248,48 @@ def tile_tubeletembedding_kernel(tc, video, W, b, pos_embed, out_0, out_1):
                 mm(banks[k][0], banks[k][1], banks[k][2])
 
         mms(0, 4)
+        x_T(1, 0)
+        x_T(1, 1)
+        late8 = []
         for i, (s, bi, nh) in enumerate(banks):
             add(s, bi, nh)
-            if s != 1:
+            if s != 1 or bi == 3:
                 st32(s, bi, NH * nh, NH * nh + NH)
             elif nh == 1:
                 st32(s, bi, 0, EMBED)
-            if i == 0:
-                w_quant(1)
-            if i < 4:
-                mms(i + 4, i + 5)
             if i == 1:
-                x_relay(1, 0, "V")
-                x_relay(1, 1, "S")
-            if i == 3:
-                x_T(1, 0)
-                x_T(1, 1)
-            if i == 4:
                 x_copy(1, 0, 0, "S")
-            if i == 5:
+            if i == 2:
                 x_copy(1, 1, 0, "S")
-                make_posb(1, 0)
+            if i == 3:
+                w_quant(1)
+                make_posb(0, 1, "V")
+                mms(4, 8)
+                g_sync(1, posb[0][:, 1023:1024].bitcast(U32))
+                make_posb(1, 1, "G")
             if i == 6:
-                make_posb(1, 1)
-            if i in (6, 7, 9, 11):
-                b2 = (6, 7, 9, 11).index(i)
-                a_quant(1, b2)
-                mms(8 + 2 * b2, 10 + 2 * b2)
-            if i == 8:
-                x_relay(1, 2, "S")
-            if i == 11:
+                a_quant_all(1)
+                x_relay(1, 2, "V")
+                mms(8, 10)
+                g_sync(2, y_t[1][2][:, 0, 0, 0:1].bitcast(U32))
+                make_posb(2, 0, "G")
+                make_posb(2, 1, "G")
+            if i in (7, 9, 11):
+                mms(i + 3, i + 5)
+            if i == 7:
                 x_T(1, 2)
-            if i == 12:
-                make_posb(2, 0)
-            if i == 13:
-                make_posb(2, 1)
+            if i == 10:
                 x_copy(1, 2, 0, "S")
-            if i == 14:
+            if i == 13:
                 a_quant(2, 0)
+            if i == 14:
                 mms(16, 18)
-            cast(s, bi, nh)
+            if i == 17:
+                cast_v(s, bi, nh)
+            else:
+                cast(s, bi, nh)
             if nh == 1:
-                st8(s, bi)
+                late8.append((i + 2, s, bi))
+            while late8 and (late8[0][0] <= i or i == 17):
+                st8(late8[0][1], late8[0][2])
+                late8.pop(0)

@@ -44,7 +44,6 @@ def tile_tubeletembedding_kernel(tc, video, W, b, pos_embed, out_0, out_1):
         bb_sb = keep.tile([P, EMBED], BF16, name="bb_sb")
         scr = keep.tile([P, 2], F32, name="scr")
         wz = keep.tile([P, P], F32, name="wz")
-        gs = keep.tile([P, 4], U32, name="gs")
         x_raw = [keep.tile([P, 2, 1536], BF16, name="x_raw%d" % t) for t in range(2)]
         w_raw = [keep.tile([P, 4, 512], BF16, name="w_raw%d" % h) for h in range(2)]
         pos_t = [keep.tile([P, EMBED], BF16, name="pos_t%d" % s) for s in range(3)]
@@ -126,9 +125,6 @@ def tile_tubeletembedding_kernel(tc, video, W, b, pos_embed, out_0, out_1):
         def a_quant_all(s):
             nc.vector.quantize_mx(out=a_c[s][:].bitcast(FP8X4), scales=a_s[s][:], in_=a_g[s][:])
 
-        def g_sync(k, words):
-            nc.gpsimd.tensor_copy(out=gs[:, k : k + 1], in_=words)
-
         def a_quant(s, bi):
             nc.vector.quantize_mx(
                 out=a_c[s][:, P * bi : P * bi + P].bitcast(FP8X4),
@@ -168,9 +164,12 @@ def tile_tubeletembedding_kernel(tc, video, W, b, pos_embed, out_0, out_1):
                 saturate=False,
             )
 
-        def st32(s, bi, lo, hi):
+        def st32(s, bi, lo, hi, pool_queue):
             d0 = o0_bh[bi, :, 8 * s : 8 * s + 8, lo:hi] if s < 2 else o0_9[:, 16:18, lo:hi]
-            nc.sync.dma_start(out=d0, in_=o32[(s, bi)][:, lo:hi])
+            if pool_queue:
+                nc.gpsimd.dma_start(out=d0, in_=o32[(s, bi)][:, lo:hi])
+            else:
+                nc.sync.dma_start(out=d0, in_=o32[(s, bi)][:, lo:hi])
 
         def st8(s, bi):
             d1 = o1_bh[bi, :, 8 * s : 8 * s + 8, :] if s < 2 else o1_9[:, 16:18, :]
@@ -232,8 +231,6 @@ def tile_tubeletembedding_kernel(tc, video, W, b, pos_embed, out_0, out_1):
             a_quant(0, bi)
         x_relay(1, 0, "V")
         x_relay(1, 1, "V")
-        g_sync(0, y_t[1][1][:, 0, 0, 0:1].bitcast(U32))
-        make_posb(1, 0, "G")
         w_copy(1, 0, "S")
         w_copy(1, 1, "S")
         x_copy(0, 1, 1, "S")
@@ -253,10 +250,11 @@ def tile_tubeletembedding_kernel(tc, video, W, b, pos_embed, out_0, out_1):
         late8 = []
         for i, (s, bi, nh) in enumerate(banks):
             add(s, bi, nh)
+            on_pool = i in (3, 5, 7, 9, 13)
             if s != 1 or bi == 3:
-                st32(s, bi, NH * nh, NH * nh + NH)
+                st32(s, bi, NH * nh, NH * nh + NH, on_pool)
             elif nh == 1:
-                st32(s, bi, 0, EMBED)
+                st32(s, bi, 0, EMBED, on_pool)
             if i == 1:
                 x_copy(1, 0, 0, "S")
             if i == 2:
@@ -265,21 +263,24 @@ def tile_tubeletembedding_kernel(tc, video, W, b, pos_embed, out_0, out_1):
                 w_quant(1)
                 make_posb(0, 1, "V")
                 mms(4, 8)
-                g_sync(1, posb[0][:, 1023:1024].bitcast(U32))
-                make_posb(1, 1, "G")
+            if i == 4:
+                make_posb(1, 0, "V")
+            if i == 5:
+                make_posb(1, 1, "V")
             if i == 6:
                 a_quant_all(1)
                 x_relay(1, 2, "V")
                 mms(8, 10)
-                g_sync(2, y_t[1][2][:, 0, 0, 0:1].bitcast(U32))
-                make_posb(2, 0, "G")
-                make_posb(2, 1, "G")
             if i in (7, 9, 11):
                 mms(i + 3, i + 5)
             if i == 7:
                 x_T(1, 2)
             if i == 10:
                 x_copy(1, 2, 0, "S")
+            if i == 11:
+                make_posb(2, 0, "V")
+            if i == 12:
+                make_posb(2, 1, "V")
             if i == 13:
                 a_quant(2, 0)
             if i == 14:

@@ -115,15 +115,9 @@ def tile_tubeletembedding_kernel(tc, video, W, b, pos_embed, out_0, out_1):
             xv = xt[(t, jp)][:].rearrange("p jj u (a il) -> p il a jj u", il=2)
             copy_on(eng, dst[:, :, qq : qq + 2, :], xv[:, il2])
 
-        def make_posb(s, nh, eng):
+        def make_posb(s, nh):
             sl = slice(NH * nh, NH * nh + NH)
-            if eng == "G":
-                nc.gpsimd.tensor_tensor(out=posb[s][:, sl], in0=pos_t[s][:, sl], in1=bb_sb[:, sl], op=ALU.add)
-            else:
-                nc.vector.tensor_tensor(out=posb[s][:, sl], in0=pos_t[s][:, sl], in1=bb_sb[:, sl], op=ALU.add)
-
-        def a_quant_all(s):
-            nc.vector.quantize_mx(out=a_c[s][:].bitcast(FP8X4), scales=a_s[s][:], in_=a_g[s][:])
+            nc.vector.tensor_tensor(out=posb[s][:, sl], in0=pos_t[s][:, sl], in1=bb_sb[:, sl], op=ALU.add)
 
         def a_quant(s, bi):
             nc.vector.quantize_mx(
@@ -164,12 +158,9 @@ def tile_tubeletembedding_kernel(tc, video, W, b, pos_embed, out_0, out_1):
                 saturate=False,
             )
 
-        def st32(s, bi, lo, hi, pool_queue):
+        def st32(s, bi, lo, hi):
             d0 = o0_bh[bi, :, 8 * s : 8 * s + 8, lo:hi] if s < 2 else o0_9[:, 16:18, lo:hi]
-            if pool_queue:
-                nc.gpsimd.dma_start(out=d0, in_=o32[(s, bi)][:, lo:hi])
-            else:
-                nc.sync.dma_start(out=d0, in_=o32[(s, bi)][:, lo:hi])
+            nc.sync.dma_start(out=d0, in_=o32[(s, bi)][:, lo:hi])
 
         def st8(s, bi):
             d1 = o1_bh[bi, :, 8 * s : 8 * s + 8, :] if s < 2 else o1_9[:, 16:18, :]
@@ -206,7 +197,7 @@ def tile_tubeletembedding_kernel(tc, video, W, b, pos_embed, out_0, out_1):
         dummy(4)
         bb_mm(0)
         bb_mm(1)
-        bb_copy(0, "S")
+        bb_copy(0, "V")
         bb_copy(1, "S")
         w_T(0, 0)
         w_T(0, 1)
@@ -215,22 +206,22 @@ def tile_tubeletembedding_kernel(tc, video, W, b, pos_embed, out_0, out_1):
         dummy(1)
         for jp in range(3):
             x_relay(0, jp, "V")
-        for jp in range(3):
-            x_T(0, jp)
-        make_posb(0, 0, "V")
+        x_T(0, 0)
+        x_T(0, 1)
+        dummy(1)
+        x_T(0, 2)
         w_quant(0)
+        make_posb(0, 0)
         x_copy(0, 0, 0, "S")
         x_copy(0, 0, 1, "S")
         x_copy(0, 1, 0, "S")
-        x_copy(0, 2, 0, "V")
+        make_posb(0, 1)
+        x_copy(0, 2, 0, "S")
         w_T(1, 0)
         dummy(1)
         w_T(1, 1)
-        dummy(1)
         for bi in range(4):
             a_quant(0, bi)
-        x_relay(1, 0, "V")
-        x_relay(1, 1, "V")
         w_copy(1, 0, "S")
         w_copy(1, 1, "S")
         x_copy(0, 1, 1, "S")
@@ -245,45 +236,45 @@ def tile_tubeletembedding_kernel(tc, video, W, b, pos_embed, out_0, out_1):
                 mm(banks[k][0], banks[k][1], banks[k][2])
 
         mms(0, 4)
-        x_T(1, 0)
-        x_T(1, 1)
         late8 = []
         for i, (s, bi, nh) in enumerate(banks):
             add(s, bi, nh)
-            on_pool = i in (3, 5, 7, 9, 13)
             if s != 1 or bi == 3:
-                st32(s, bi, NH * nh, NH * nh + NH, on_pool)
+                st32(s, bi, NH * nh, NH * nh + NH)
             elif nh == 1:
-                st32(s, bi, 0, EMBED, on_pool)
-            if i == 1:
-                x_copy(1, 0, 0, "S")
-            if i == 2:
-                x_copy(1, 1, 0, "S")
-            if i == 3:
+                st32(s, bi, 0, EMBED)
+            if i == 0:
                 w_quant(1)
-                make_posb(0, 1, "V")
-                mms(4, 8)
+            if i < 4:
+                mms(i + 4, i + 5)
+            if i == 1:
+                x_relay(1, 0, "V")
+                x_relay(1, 1, "S")
+            if i == 3:
+                x_T(1, 0)
+                x_T(1, 1)
             if i == 4:
-                make_posb(1, 0, "V")
+                x_copy(1, 0, 0, "S")
             if i == 5:
-                make_posb(1, 1, "V")
+                x_copy(1, 1, 0, "S")
+                make_posb(1, 0)
             if i == 6:
-                a_quant_all(1)
-                x_relay(1, 2, "V")
-                mms(8, 10)
-            if i in (7, 9, 11):
-                mms(i + 3, i + 5)
-            if i == 7:
-                x_T(1, 2)
-            if i == 10:
-                x_copy(1, 2, 0, "S")
+                make_posb(1, 1)
+            if i in (6, 7, 9, 11):
+                b2 = (6, 7, 9, 11).index(i)
+                a_quant(1, b2)
+                mms(8 + 2 * b2, 10 + 2 * b2)
+            if i == 8:
+                x_relay(1, 2, "S")
             if i == 11:
-                make_posb(2, 0, "V")
+                x_T(1, 2)
             if i == 12:
-                make_posb(2, 1, "V")
+                make_posb(2, 0)
             if i == 13:
-                a_quant(2, 0)
+                make_posb(2, 1)
+                x_copy(1, 2, 0, "S")
             if i == 14:
+                a_quant(2, 0)
                 mms(16, 18)
             if i == 17:
                 cast_v(s, bi, nh)

@@ -170,6 +170,12 @@ def tile_tubeletembedding_kernel(tc, video, W, b, pos_embed, out_0, out_1):
             for k in range(n):
                 nc.tensor.matmul(junk[:, 0:P], lhsT=wz[:], rhs=wz[:], start=True, stop=True)
 
+        def keep_warm(s, bi, nh):
+            jt = tps.tile([P, 2, 2, P], F32, name="jt", tag="tp")
+            nc.tensor.matmul(
+                jt[:, 0, 0, :], lhsT=wz[:], rhs=o32[(s, bi)][:, NH * nh : NH * nh + P], start=True, stop=True
+            )
+
         make_identity(nc, ident[:])
         nc.gpsimd.memset(ones[:], 1.0)
         nc.gpsimd.memset(scr[:], 0.0)
@@ -253,10 +259,7 @@ def tile_tubeletembedding_kernel(tc, video, W, b, pos_embed, out_0, out_1):
             if i == 3:
                 x_T(1, 0)
                 x_T(1, 1)
-            if i == 4:
-                x_copy(1, 0, 0, "S")
             if i == 5:
-                x_copy(1, 1, 0, "S")
                 make_posb(1, 0)
             if i == 6:
                 make_posb(1, 1)
@@ -268,6 +271,8 @@ def tile_tubeletembedding_kernel(tc, video, W, b, pos_embed, out_0, out_1):
                 x_relay(1, 2, "S")
             if i == 11:
                 x_T(1, 2)
+            if i in (4, 5, 6, 7, 12, 13):
+                keep_warm(s, bi, nh)
             if i == 12:
                 make_posb(2, 0)
             if i == 13:
@@ -280,6 +285,10 @@ def tile_tubeletembedding_kernel(tc, video, W, b, pos_embed, out_0, out_1):
                 cast_v(s, bi, nh)
             else:
                 cast(s, bi, nh)
+            if i == 4:
+                x_copy(1, 0, 0, "S")
+            if i == 5:
+                x_copy(1, 1, 0, "S")
             if nh == 1:
                 late8.append((i + 2, s, bi))
             while late8 and (late8[0][0] <= i or i == 17):

@@ -43,10 +43,13 @@ def tile_tubeletembedding_kernel(tc, video, W, b, pos_embed, out_0, out_1):
         brow = keep.tile([P, EMBED], BF16, name="brow")
         bb_sb = keep.tile([P, EMBED], BF16, name="bb_sb")
         scr = keep.tile([P, 2], F32, name="scr")
+        gate = keep.tile([P, 1], U32, name="gate")
         wz = keep.tile([P, P], F32, name="wz")
         x_raw = [keep.tile([P, 2, 1536], BF16, name="x_raw%d" % t) for t in range(2)]
         w_raw = [keep.tile([P, 4, 512], BF16, name="w_raw%d" % h) for h in range(2)]
-        pos_t = [keep.tile([P, EMBED], BF16, name="pos_t%d" % s) for s in range(3)]
+        pos_t = [keep.tile([P, EMBED], BF16, name="pos_t%d" % s) for s in range(2)]
+        prow = keep.tile([P, EMBED], BF16, name="prow")
+        sel = keep.tile([P, P], BF16, name="sel")
         posb = [keep.tile([P, EMBED], F32, name="posb%d" % s) for s in range(3)]
         y_t = [[keep.tile([P, 2, 2, P], F32, name="y%d_%d" % (t, jp)) for jp in range(3)] for t in range(2)]
         w_g = [keep.tile([P, 4 * NH], BF16, name="w_g%d" % h, align_bytes=64) for h in range(2)]
@@ -91,6 +94,13 @@ def tile_tubeletembedding_kernel(tc, video, W, b, pos_embed, out_0, out_1):
         def bb_copy(nh, eng):
             copy_on(eng, bb_sb[:, NH * nh : NH * nh + NH], bbp[nh][:])
 
+        def p2_mm(nh):
+            bbp[2 + nh] = tps.tile([P, NH], F32, name="p2p", tag="tp")
+            nc.tensor.matmul(bbp[2 + nh][:], lhsT=sel[:], rhs=prow[:, NH * nh : NH * nh + NH], start=True, stop=True)
+
+        def p2_copy(nh, eng):
+            copy_on(eng, posb[2][:, NH * nh : NH * nh + NH], bbp[2 + nh][:])
+
         def x_relay(t, jp, eng):
             xw = x_raw[t][:].bitcast(F32).rearrange(
                 "p ts (py j wq u) -> p j u (ts py) wq", py=16, j=6, wq=4, u=2
@@ -115,15 +125,17 @@ def tile_tubeletembedding_kernel(tc, video, W, b, pos_embed, out_0, out_1):
             xv = xt[(t, jp)][:].rearrange("p jj u (a il) -> p il a jj u", il=2)
             copy_on(eng, dst[:, :, qq : qq + 2, :], xv[:, il2])
 
-        def make_posb(s, nh):
+        def make_posb(s, nh, eng="V"):
             sl = slice(NH * nh, NH * nh + NH)
-            nc.vector.tensor_tensor(out=posb[s][:, sl], in0=pos_t[s][:, sl], in1=bb_sb[:, sl], op=ALU.add)
+            eg = nc.vector if eng == "V" else nc.gpsimd
+            bb = bbp[nh][:] if eng == "V" else bb_sb[:, sl]
+            eg.tensor_tensor(out=posb[s][:, sl], in0=pos_t[s][:, sl], in1=bb, op=ALU.add)
 
-        def a_quant(s, bi):
+        def a_quant(s, bi, n=1):
             nc.vector.quantize_mx(
-                out=a_c[s][:, P * bi : P * bi + P].bitcast(FP8X4),
-                scales=a_s[s][:, P * bi : P * bi + P],
-                in_=a_g[s][:, 4 * P * bi : 4 * P * bi + 4 * P],
+                out=a_c[s][:, P * bi : P * (bi + n)].bitcast(FP8X4),
+                scales=a_s[s][:, P * bi : P * (bi + n)],
+                in_=a_g[s][:, 4 * P * bi : 4 * P * (bi + n)],
             )
 
         def mm(s, bi, nh):
@@ -177,61 +189,65 @@ def tile_tubeletembedding_kernel(tc, video, W, b, pos_embed, out_0, out_1):
             )
 
         make_identity(nc, ident[:])
-        nc.gpsimd.memset(ones[:], 1.0)
-        nc.gpsimd.memset(scr[:], 0.0)
+        nc.gpsimd.memset(prow[:].bitcast(F32), 0.0)
+        nc.gpsimd.memset(sel[:], 0.0)
+        for c in range(4):
+            nc.gpsimd.tensor_copy(out=sel[:, 32 * c : 32 * c + 32], in_=ident[:, 0:32])
+        nc.gpsimd.memset(sel[32:33, :], 1.0)
         nc.vector.memset(wz[:], 0.0)
         nc.vector.memset(brow[:].bitcast(F32), 0.0)
+        nc.vector.memset(ones[:], 1.0)
+        nc.vector.memset(scr[:], 0.0)
         nc.vector.memset(x_raw[1][:].bitcast(F32), 0.0)
 
         ctx.enter_context(tc.manual_schedule())
+        brw = b.rearrange("(o e) -> o e", o=1)
         nc.scalar.activation(out=scr[:, 1:2], in_=scr[:, 0:1], func=ACT.Copy, scale=1.0)
 
-        nc.sync.dma_start(out=w_raw[0][:].rearrange("p e k -> p (e k)"), in_=wv[0])
-        nc.sync.dma_start(out=brow[0:1, :], in_=b.rearrange("(o e) -> o e", o=1))
+        nc.sync.dma_start(out=w_raw[0][:, 0:2, :].rearrange("p e k -> p (e k)"), in_=wv[0, :, 0:1024])
         for ts in range(2):
             for il in range(2):
                 nc.sync.dma_start(out=x_raw[0][il::2, ts, :], in_=vid[ts, il])
+        nc.sync.dma_start(out=brow[0:1, :], in_=brw)
+        nc.sync.dma_start(out=w_raw[0][:, 2:4, :].rearrange("p e k -> p (e k)"), in_=wv[0, :, 1024:2048])
         nc.sync.dma_start(out=pos_t[0][:], in_=pv[:, 0:8, :])
         nc.sync.dma_start(out=w_raw[1][:].rearrange("p e k -> p (e k)"), in_=wv[1])
         for ts in range(2):
             nc.sync.dma_start(out=x_raw[1][0::2, ts, :], in_=vid[ts, 2])
         nc.sync.dma_start(out=pos_t[1][:], in_=pv[:, 8:16, :])
-        for bi in range(4):
-            nc.sync.dma_start(out=pos_t[2][32 * bi : 32 * bi + 32, :], in_=pv[:, 16:18, :])
+        nc.sync.dma_start(out=prow[0:32, :], in_=pv[:, 16:18, :])
+        nc.sync.dma_start(out=prow[32:33, :], in_=brw)
 
         junk = accs.tile([P, NH], F32, name="junk", tag="acc")
         dummy(4)
-        bb_mm(0)
-        bb_mm(1)
-        bb_copy(0, "V")
-        bb_copy(1, "S")
         w_T(0, 0)
-        w_T(0, 1)
+        dummy(1)
+        bb_mm(0)
         w_copy(0, 0, "S")
-        w_copy(0, 1, "S")
-        dummy(1)
-        for jp in range(3):
-            x_relay(0, jp, "V")
+        x_relay(0, 0, "V")
+        x_relay(0, 1, "V")
+        x_relay(0, 2, "V")
         x_T(0, 0)
+        w_T(0, 1)
         x_T(0, 1)
-        dummy(1)
         x_T(0, 2)
-        w_quant(0)
+        bb_mm(1)
+        dummy(1)
+        bb_copy(0, "S")
         make_posb(0, 0)
         x_copy(0, 0, 0, "S")
-        x_copy(0, 0, 1, "S")
+        x_copy(0, 0, 1, "V")
+        w_copy(0, 1, "S")
         x_copy(0, 1, 0, "S")
-        make_posb(0, 1)
         x_copy(0, 2, 0, "S")
-        w_T(1, 0)
-        dummy(1)
-        w_T(1, 1)
-        for bi in range(4):
-            a_quant(0, bi)
-        w_copy(1, 0, "S")
-        w_copy(1, 1, "S")
+        bb_copy(1, "S")
+        make_posb(0, 1, "G")
         x_copy(0, 1, 1, "S")
         x_copy(0, 2, 1, "S")
+        w_quant(0)
+        a_quant(0, 0)
+        a_quant(0, 1)
+        a_quant(0, 2, 2)
 
         banks = [(0, bi, nh) for nh in range(2) for bi in range(4)]
         banks += [(1, bi, nh) for bi in range(4) for nh in range(2)]
@@ -241,54 +257,63 @@ def tile_tubeletembedding_kernel(tc, video, W, b, pos_embed, out_0, out_1):
             for k in range(lo, hi):
                 mm(banks[k][0], banks[k][1], banks[k][2])
 
-        mms(0, 4)
+        mms(0, 2)
+        w_T(1, 0)
+        w_T(1, 1)
+        mms(2, 4)
+        w_copy(1, 0, "S")
+        w_copy(1, 1, "S")
         late8 = []
+        on_v = (11, 14, 17)
         for i, (s, bi, nh) in enumerate(banks):
             add(s, bi, nh)
-            if s != 1 or bi == 3:
+            if i < 8 or i > 13:
                 st32(s, bi, NH * nh, NH * nh + NH)
             elif nh == 1:
                 st32(s, bi, 0, EMBED)
-            if i == 0:
-                w_quant(1)
-            if i < 4:
-                mms(i + 4, i + 5)
-            if i == 1:
-                x_relay(1, 0, "V")
-                x_relay(1, 1, "S")
+            if i - 1 in on_v:
+                cast_v(banks[i - 1][0], banks[i - 1][1], banks[i - 1][2])
+            if i in (1, 2):
+                keep_warm(s, bi, nh)
             if i == 3:
+                w_quant(1)
+                nc.gpsimd.tensor_copy(out=gate[:], in_=w_c[1][:, 0:1])
+                make_posb(1, 0, "G")
+                make_posb(1, 1, "G")
+                x_relay(1, 0, "V")
+                x_relay(1, 2, "V")
+                mms(4, 8)
                 x_T(1, 0)
                 x_T(1, 1)
-            if i == 5:
-                make_posb(1, 0)
-            if i == 6:
-                make_posb(1, 1)
-            if i in (6, 7, 9, 11):
-                b2 = (6, 7, 9, 11).index(i)
-                a_quant(1, b2)
-                mms(8 + 2 * b2, 10 + 2 * b2)
-            if i == 8:
-                x_relay(1, 2, "S")
-            if i == 11:
                 x_T(1, 2)
-            if i in (4, 5, 6, 7, 12, 13):
-                keep_warm(s, bi, nh)
+            if i == 5:
+                p2_mm(0)
+                p2_mm(1)
+            if i in (6, 7):
+                a_quant(1, 2 * i - 12, 2)
+                mms(4 * i - 16, 4 * i - 14)
+            if i in (8, 9, 10, 11):
+                mms(i + 2 if i < 10 else i + 4, i + 3 if i < 10 else i + 5)
             if i == 12:
-                make_posb(2, 0)
-            if i == 13:
-                make_posb(2, 1)
-                x_copy(1, 2, 0, "S")
-            if i == 14:
                 a_quant(2, 0)
-                mms(16, 18)
+                mms(16, 17)
+            if i == 13:
+                mms(17, 18)
             if i == 17:
                 cast_v(s, bi, nh)
-            else:
+            elif i not in on_v:
                 cast(s, bi, nh)
-            if i == 4:
+            if i == 0:
+                x_relay(1, 1, "S")
+            if i == 3:
                 x_copy(1, 0, 0, "S")
-            if i == 5:
                 x_copy(1, 1, 0, "S")
+            if i == 7:
+                x_copy(1, 2, 0, "S")
+            if i == 8:
+                p2_copy(0, "S")
+            if i == 10:
+                p2_copy(1, "S")
             if nh == 1:
                 late8.append((i + 2, s, bi))
             while late8 and (late8[0][0] <= i or i == 17):

@@ -15,6 +15,7 @@ ALU = mybir.AluOpType
 P = 128
 EMBED = 1024
 NH = 512
+ROOM = 320
 Y_SCALE = 170.0
 FLOPS = 2 * 1152 * 512 * 1024
 
@@ -22,43 +23,38 @@ FLOPS = 2 * 1152 * 512 * 1024
 def tile_tubeletembedding_kernel(tc, video, W, b, pos_embed, out_0, out_1):
     nc = tc.nc
 
-    vid = video[:, :, 0, :, :].rearrange(
-        "b (d ts) (ih il py) x -> ts il (b d) ih (py x)", ts=2, ih=2, il=3
-    )
+    vid = video[:, :, 0, :, :].rearrange("b (d ts) (i y) x -> ts (b d) i (y x)", ts=2, y=16)
     wv = W.rearrange("(h p e4) k -> h p (e4 k)", p=P, e4=4)
-    pv = pos_embed[0].rearrange("(a q) e -> a q e", q=18)
-    o0_bh = out_0.rearrange("b (a q) e -> b a q e", q=18)
-    o1_bh = out_1.rearrange("b (a q) e -> b a q e", q=18)
-    o0_9 = out_0.rearrange("b (a q) e -> (b a) q e", q=18)
-    o1_9 = out_1.rearrange("b (a q) e -> (b a) q e", q=18)
+    pos = pos_embed[0]
+    rest0 = out_0[:, 256:288, :].rearrange("b m x -> m b x")
+    rest1 = out_1[:, 256:288, :].rearrange("b m x -> m b x")
 
     with ExitStack() as ctx:
         keep = ctx.enter_context(tc.tile_pool(name="keep", bufs=1))
         outp = ctx.enter_context(tc.tile_pool(name="outp", bufs=9))
-        tps = ctx.enter_context(tc.psum_pool(name="tps", bufs=4))
-        accs = ctx.enter_context(tc.psum_pool(name="accs", bufs=4))
+        tps = ctx.enter_context(tc.psum_pool(name="tps", bufs=3))
+        accs = ctx.enter_context(tc.psum_pool(name="accs", bufs=3))
+        bbs = ctx.enter_context(tc.psum_pool(name="bbs", bufs=2))
 
         ident = keep.tile([P, P], F32, name="ident")
         ones = keep.tile([P, P], BF16, name="ones")
         brow = keep.tile([P, EMBED], BF16, name="brow")
-        bb_sb = keep.tile([P, EMBED], BF16, name="bb_sb")
-        scr = keep.tile([P, 2], F32, name="scr")
-        gate = keep.tile([P, 1], U32, name="gate")
-        wz = keep.tile([P, P], F32, name="wz")
-        x_raw = [keep.tile([P, 2, 1536], BF16, name="x_raw%d" % t) for t in range(2)]
-        w_raw = [keep.tile([P, 4, 512], BF16, name="w_raw%d" % h) for h in range(2)]
-        pos_t = [keep.tile([P, EMBED], BF16, name="pos_t%d" % s) for s in range(2)]
         prow = keep.tile([P, EMBED], BF16, name="prow")
         sel = keep.tile([P, P], BF16, name="sel")
+        scr = keep.tile([P, 2], F32, name="scr")
+        wz = keep.tile([P, P], F32, name="wz")
+        x_raw = [keep.tile([P, 2, 1536], BF16, name="x_raw%d" % h) for h in range(2)]
+        w_raw = [keep.tile([P, 4, 512], BF16, name="w_raw%d" % h) for h in range(2)]
+        pos_t = [keep.tile([P, EMBED], BF16, name="pos_t%d" % s) for s in range(2)]
         posb = [keep.tile([P, EMBED], F32, name="posb%d" % s) for s in range(3)]
-        y_t = [[keep.tile([P, 2, 2, P], F32, name="y%d_%d" % (t, jp)) for jp in range(3)] for t in range(2)]
+        y_t = [[keep.tile([P, 2, 2, P], F32, name="y%d_%d" % (h, jp)) for jp in range(3)] for h in range(2)]
         w_g = [keep.tile([P, 4 * NH], BF16, name="w_g%d" % h, align_bytes=64) for h in range(2)]
         w_c = [keep.tile([P, NH], U32, name="w_c%d" % h, align_bytes=64) for h in range(2)]
         w_s = [keep.tile([P, NH], U8, name="w_s%d" % h, align_bytes=64) for h in range(2)]
-        a_cols = [512, 512, 128]
-        a_g = [keep.tile([P, 4 * a_cols[s]], BF16, name="a_g%d" % s, align_bytes=64) for s in range(3)]
-        a_c = [keep.tile([P, a_cols[s]], U32, name="a_c%d" % s, align_bytes=64) for s in range(3)]
-        a_s = [keep.tile([P, a_cols[s]], U8, name="a_s%d" % s, align_bytes=64) for s in range(3)]
+        a_cols = [2 * ROOM, 2 * ROOM, P]
+        a_g = [keep.tile([P, 4 * a_cols[h]], BF16, name="a_g%d" % h, align_bytes=64) for h in range(3)]
+        a_c = [keep.tile([P, a_cols[h]], U32, name="a_c%d" % h, align_bytes=64) for h in range(3)]
+        a_s = [keep.tile([P, a_cols[h]], U8, name="a_s%d" % h, align_bytes=64) for h in range(3)]
 
         wt = {}
         xt = {}
@@ -88,62 +84,61 @@ def tile_tubeletembedding_kernel(tc, video, W, b, pos_embed, out_0, out_1):
             nc.vector.quantize_mx(out=w_c[h][:].bitcast(FP8X4), scales=w_s[h][:], in_=w_g[h][:])
 
         def bb_mm(nh):
-            bbp[nh] = accs.tile([P, NH], F32, name="bbp", tag="acc")
+            bbp[nh] = bbs.tile([P, NH], F32, name="bbp", tag="bb")
             nc.tensor.matmul(bbp[nh][:], lhsT=ones[:], rhs=brow[:, NH * nh : NH * nh + NH], start=True, stop=True)
 
-        def bb_copy(nh, eng):
-            copy_on(eng, bb_sb[:, NH * nh : NH * nh + NH], bbp[nh][:])
-
         def p2_mm(nh):
-            bbp[2 + nh] = tps.tile([P, NH], F32, name="p2p", tag="tp")
+            bbp[2 + nh] = bbs.tile([P, NH], F32, name="p2p", tag="bb")
             nc.tensor.matmul(bbp[2 + nh][:], lhsT=sel[:], rhs=prow[:, NH * nh : NH * nh + NH], start=True, stop=True)
 
         def p2_copy(nh, eng):
             copy_on(eng, posb[2][:, NH * nh : NH * nh + NH], bbp[2 + nh][:])
 
-        def x_relay(t, jp, eng):
-            xw = x_raw[t][:].bitcast(F32).rearrange(
-                "p ts (py j wq u) -> p j u (ts py) wq", py=16, j=6, wq=4, u=2
-            )
+        def x_relay(h, jp, eng):
+            xw = x_raw[h][:].bitcast(F32).rearrange("p ts (py j wq u) -> p j u (ts py) wq", py=16, j=6, wq=4, u=2)
             copy_on(
                 eng,
-                y_t[t][jp][:].rearrange("p jj u (tp wq) -> p jj u tp wq", wq=4),
+                y_t[h][jp][:].rearrange("p jj u (tp wq) -> p jj u tp wq", wq=4),
                 xw[:, 2 * jp : 2 * jp + 2],
             )
 
-        def x_T(t, jp):
-            xt[(t, jp)] = tps.tile([P, 2, 2, P], F32, name="xt", tag="tp")
+        def x_T(h, jp):
+            xt[(h, jp)] = tps.tile([P, 2, 2, P], F32, name="xt", tag="tp")
             for jj in range(2):
                 for u in range(2):
-                    nc.tensor.transpose(xt[(t, jp)][:, jj, u, :], y_t[t][jp][:, jj, u, :], ident[:])
+                    nc.tensor.transpose(xt[(h, jp)][:, jj, u, :], y_t[h][jp][:, jj, u, :], ident[:])
 
-        def x_copy(t, jp, il2, eng):
-            il = il2 if t == 0 else 2
-            q = 6 * il + 2 * jp
-            s, qq, nq = (q // 8, q % 8, 8) if q < 16 else (2, q - 16, 2)
-            dst = a_g[s][:].bitcast(F32).rearrange("p (a q u) -> p a q u", q=nq, u=2)
-            xv = xt[(t, jp)][:].rearrange("p jj u (a il) -> p il a jj u", il=2)
-            copy_on(eng, dst[:, :, qq : qq + 2, :], xv[:, il2])
+        def x_copy(h, jp, lo, hi, eng):
+            dst = a_g[h][:].bitcast(F32).rearrange("p (b c) -> p b c", b=2)[:, :, 0:576]
+            dst = dst.rearrange("p b (st j3 jj u) -> p b st j3 jj u", j3=3, jj=2, u=2)
+            src = xt[(h, jp)][:, :, :, 0:96].rearrange("p jj u (b st) -> p b st jj u", b=2)
+            copy_on(eng, dst[:, :, lo:hi, jp], src[:, :, lo:hi])
 
-        def make_posb(s, nh, eng="V"):
+        def x_rest(h, jp, eng):
+            n = 6 if jp == 2 else 5
+            dst = a_g[2][:].bitcast(F32).rearrange("p (pr jj b u) -> p b pr jj u", b=4, jj=2, u=2)
+            src = xt[(h, jp)][:, :, :, 0:96].rearrange("p jj u (b st) -> p b st jj u", b=2)
+            copy_on(eng, dst[:, 2 * h : 2 * h + 2, (jp + 1) % 3 : 16 : 3], src[:, :, 48 - n : 48])
+
+        def make_posb(s, nh):
             sl = slice(NH * nh, NH * nh + NH)
-            eg = nc.vector if eng == "V" else nc.gpsimd
-            bb = bbp[nh][:] if eng == "V" else bb_sb[:, sl]
-            eg.tensor_tensor(out=posb[s][:, sl], in0=pos_t[s][:, sl], in1=bb, op=ALU.add)
+            nc.vector.tensor_tensor(out=posb[s][:, sl], in0=pos_t[s][:, sl], in1=bbp[nh][:], op=ALU.add)
 
-        def a_quant(s, bi, n=1):
+        def a_quant(s, bi):
+            h, k = (2, 0) if s == 2 else (bi // 2, ROOM * (bi % 2) + P * s)
             nc.vector.quantize_mx(
-                out=a_c[s][:, P * bi : P * (bi + n)].bitcast(FP8X4),
-                scales=a_s[s][:, P * bi : P * (bi + n)],
-                in_=a_g[s][:, 4 * P * bi : 4 * P * (bi + n)],
+                out=a_c[h][:, k : k + P].bitcast(FP8X4),
+                scales=a_s[h][:, k : k + P],
+                in_=a_g[h][:, 4 * k : 4 * k + 4 * P],
             )
 
         def mm(s, bi, nh):
+            h, k = (2, 0) if s == 2 else (bi // 2, ROOM * (bi % 2) + P * s)
             acc[(s, bi, nh)] = accs.tile([P, NH], F32, name="acc", tag="acc")
             nc.tensor.matmul_mx(
                 out=acc[(s, bi, nh)][:],
-                lhsT=a_c[s][:, P * bi : P * bi + P].bitcast(FP8X4),
-                lhsT_scale=a_s[s][:, P * bi : P * bi + P],
+                lhsT=a_c[h][:, k : k + P].bitcast(FP8X4),
+                lhsT_scale=a_s[h][:, k : k + P],
                 rhs=w_c[nh][:].bitcast(FP8X4),
                 rhs_scale=w_s[nh][:],
                 start=True,
@@ -171,11 +166,11 @@ def tile_tubeletembedding_kernel(tc, video, W, b, pos_embed, out_0, out_1):
             )
 
         def st32(s, bi, lo, hi):
-            d0 = o0_bh[bi, :, 8 * s : 8 * s + 8, lo:hi] if s < 2 else o0_9[:, 16:18, lo:hi]
+            d0 = out_0[bi, P * s : P * s + P, lo:hi] if s < 2 else rest0[:, :, lo:hi]
             nc.sync.dma_start(out=d0, in_=o32[(s, bi)][:, lo:hi])
 
         def st8(s, bi):
-            d1 = o1_bh[bi, :, 8 * s : 8 * s + 8, :] if s < 2 else o1_9[:, 16:18, :]
+            d1 = out_1[bi, P * s : P * s + P, :] if s < 2 else rest1
             nc.sync.dma_start(out=d1, in_=o8[(s, bi)][:].bitcast(U8))
 
         def dummy(n):
@@ -191,14 +186,15 @@ def tile_tubeletembedding_kernel(tc, video, W, b, pos_embed, out_0, out_1):
         make_identity(nc, ident[:])
         nc.gpsimd.memset(prow[:].bitcast(F32), 0.0)
         nc.gpsimd.memset(sel[:], 0.0)
-        for c in range(4):
-            nc.gpsimd.tensor_copy(out=sel[:, 32 * c : 32 * c + 32], in_=ident[:, 0:32])
+        for bi in range(4):
+            nc.gpsimd.tensor_copy(out=sel[:, bi::4], in_=ident[:, 0:32])
         nc.gpsimd.memset(sel[32:33, :], 1.0)
         nc.vector.memset(wz[:], 0.0)
         nc.vector.memset(brow[:].bitcast(F32), 0.0)
         nc.vector.memset(ones[:], 1.0)
         nc.vector.memset(scr[:], 0.0)
-        nc.vector.memset(x_raw[1][:].bitcast(F32), 0.0)
+        nc.vector.memset(x_raw[0][96:128].bitcast(F32), 0.0)
+        nc.gpsimd.memset(x_raw[1][96:128].bitcast(F32), 0.0)
 
         ctx.enter_context(tc.manual_schedule())
         brw = b.rearrange("(o e) -> o e", o=1)
@@ -206,52 +202,49 @@ def tile_tubeletembedding_kernel(tc, video, W, b, pos_embed, out_0, out_1):
 
         nc.sync.dma_start(out=w_raw[0][:, 0:2, :].rearrange("p e k -> p (e k)"), in_=wv[0, :, 0:1024])
         for ts in range(2):
-            for il in range(2):
-                nc.sync.dma_start(out=x_raw[0][il::2, ts, :], in_=vid[ts, il])
+            nc.sync.dma_start(out=x_raw[0][0:96, ts, :], in_=vid[ts, 0:16])
         nc.sync.dma_start(out=brow[0:1, :], in_=brw)
         nc.sync.dma_start(out=w_raw[0][:, 2:4, :].rearrange("p e k -> p (e k)"), in_=wv[0, :, 1024:2048])
-        nc.sync.dma_start(out=pos_t[0][:], in_=pv[:, 0:8, :])
+        nc.sync.dma_start(out=pos_t[0][:], in_=pos[0:128, :])
+        nc.sync.dma_start(out=pos_t[1][:], in_=pos[128:256, :])
         nc.sync.dma_start(out=w_raw[1][:].rearrange("p e k -> p (e k)"), in_=wv[1])
         for ts in range(2):
-            nc.sync.dma_start(out=x_raw[1][0::2, ts, :], in_=vid[ts, 2])
-        nc.sync.dma_start(out=pos_t[1][:], in_=pv[:, 8:16, :])
-        nc.sync.dma_start(out=prow[0:32, :], in_=pv[:, 16:18, :])
+            nc.sync.dma_start(out=x_raw[1][0:96, ts, :], in_=vid[ts, 16:32])
+        nc.sync.dma_start(out=prow[0:32, :], in_=pos[256:288, :])
         nc.sync.dma_start(out=prow[32:33, :], in_=brw)
 
         junk = accs.tile([P, NH], F32, name="junk", tag="acc")
         dummy(4)
         w_T(0, 0)
-        dummy(1)
         bb_mm(0)
+        bb_mm(1)
+        for jp in range(3):
+            x_relay(0, jp, "V")
         w_copy(0, 0, "S")
-        x_relay(0, 0, "V")
-        x_relay(0, 1, "V")
-        x_relay(0, 2, "V")
         x_T(0, 0)
         w_T(0, 1)
-        x_T(0, 1)
-        x_T(0, 2)
-        bb_mm(1)
-        dummy(1)
-        bb_copy(0, "S")
-        make_posb(0, 0)
-        x_copy(0, 0, 0, "S")
-        x_copy(0, 0, 1, "V")
+        x_copy(0, 0, 0, 48, "S")
+        x_rest(0, 0, "S")
         w_copy(0, 1, "S")
-        x_copy(0, 1, 0, "S")
-        x_copy(0, 2, 0, "S")
-        bb_copy(1, "S")
-        make_posb(0, 1, "G")
-        x_copy(0, 1, 1, "S")
-        x_copy(0, 2, 1, "S")
+        x_T(0, 1)
+        dummy(1)
+        x_T(0, 2)
+        make_posb(0, 0)
+        x_copy(0, 1, 0, 22, "V")
+        x_copy(0, 2, 0, 22, "S")
         w_quant(0)
         a_quant(0, 0)
         a_quant(0, 1)
-        a_quant(0, 2, 2)
+        dummy(1)
+        x_copy(0, 1, 22, 48, "S")
+        x_copy(0, 2, 22, 48, "S")
+        x_rest(0, 1, "S")
+        x_rest(0, 2, "S")
+        make_posb(1, 0)
 
-        banks = [(0, bi, nh) for nh in range(2) for bi in range(4)]
-        banks += [(1, bi, nh) for bi in range(4) for nh in range(2)]
-        banks += [(2, 0, 0), (2, 0, 1)]
+        banks = [(0, 0, 0), (0, 1, 0), (1, 0, 0), (1, 1, 0), (0, 0, 1), (0, 1, 1), (1, 0, 1), (1, 1, 1)]
+        banks += [(0, 2, 0), (0, 2, 1), (0, 3, 0), (0, 3, 1), (1, 2, 0), (1, 2, 1), (2, 0, 0), (2, 0, 1)]
+        banks += [(1, 3, 0), (1, 3, 1)]
 
         def mms(lo, hi):
             for k in range(lo, hi):
@@ -260,56 +253,68 @@ def tile_tubeletembedding_kernel(tc, video, W, b, pos_embed, out_0, out_1):
         mms(0, 2)
         w_T(1, 0)
         w_T(1, 1)
-        mms(2, 4)
         w_copy(1, 0, "S")
         w_copy(1, 1, "S")
         late8 = []
-        on_v = (11, 14, 17)
         for i, (s, bi, nh) in enumerate(banks):
             add(s, bi, nh)
-            if i < 8 or i > 13:
+            if i < 8 or i > 15:
                 st32(s, bi, NH * nh, NH * nh + NH)
             elif nh == 1:
                 st32(s, bi, 0, EMBED)
-            if i - 1 in on_v:
-                cast_v(banks[i - 1][0], banks[i - 1][1], banks[i - 1][2])
+            if i == 0:
+                a_quant(1, 0)
+                a_quant(1, 1)
+                mms(2, 4)
             if i in (1, 2):
                 keep_warm(s, bi, nh)
+            if i == 2:
+                x_relay(1, 0, "V")
             if i == 3:
                 w_quant(1)
-                nc.gpsimd.tensor_copy(out=gate[:], in_=w_c[1][:, 0:1])
-                make_posb(1, 0, "G")
-                make_posb(1, 1, "G")
-                x_relay(1, 0, "V")
-                x_relay(1, 2, "V")
-                mms(4, 8)
+                make_posb(0, 1)
+                mms(4, 7)
                 x_T(1, 0)
+            if i == 4:
+                mms(7, 8)
+                x_relay(1, 1, "V")
                 x_T(1, 1)
-                x_T(1, 2)
             if i == 5:
+                make_posb(1, 1)
+                x_relay(1, 2, "V")
+                x_T(1, 2)
                 p2_mm(0)
                 p2_mm(1)
-            if i in (6, 7):
-                a_quant(1, 2 * i - 12, 2)
-                mms(4 * i - 16, 4 * i - 14)
-            if i in (8, 9, 10, 11):
-                mms(i + 2 if i < 10 else i + 4, i + 3 if i < 10 else i + 5)
-            if i == 12:
+            if i == 7:
+                a_quant(0, 2)
+                mms(8, 10)
+            if i == 8:
+                a_quant(0, 3)
+                mms(10, 11)
+            if i == 9:
+                a_quant(1, 2)
+                mms(11, 12)
+            if i in (10, 11, 12, 13, 14):
+                mms(i + 2, i + 3)
+            if i == 10:
                 a_quant(2, 0)
-                mms(16, 17)
-            if i == 13:
+            if i == 11:
+                a_quant(1, 3)
+            if i == 15:
                 mms(17, 18)
             if i == 17:
                 cast_v(s, bi, nh)
-            elif i not in on_v:
+            else:
                 cast(s, bi, nh)
-            if i == 0:
-                x_relay(1, 1, "S")
             if i == 3:
-                x_copy(1, 0, 0, "S")
-                x_copy(1, 1, 0, "S")
+                x_copy(1, 0, 0, 48, "S")
+            if i == 4:
+                x_copy(1, 1, 0, 48, "S")
+            if i == 5:
+                x_copy(1, 2, 0, 48, "S")
             if i == 7:
-                x_copy(1, 2, 0, "S")
+                for jp in range(3):
+                    x_rest(1, jp, "S")
             if i == 8:
                 p2_copy(0, "S")
             if i == 10:

@@ -132,9 +132,11 @@ def tile_tubeletembedding_kernel(tc, video, W, b, pos_embed, out_0, out_1):
                 in_=a_g[h][:, 4 * k : 4 * k + 4 * P],
             )
 
-        def mm(s, bi, nh):
+        def mm(s, bi, nh, warm=0):
             h, k = (2, 0) if s == 2 else (bi // 2, ROOM * (bi % 2) + P * s)
             acc[(s, bi, nh)] = accs.tile([P, NH], F32, name="acc", tag="acc")
+            for d in range(warm):
+                nc.tensor.matmul(acc[(s, bi, nh)][:, 0:P], lhsT=wz[:], rhs=wz[:], start=True, stop=True)
             nc.tensor.matmul_mx(
                 out=acc[(s, bi, nh)][:],
                 lhsT=a_c[h][:, k : k + P].bitcast(FP8X4),
@@ -176,12 +178,6 @@ def tile_tubeletembedding_kernel(tc, video, W, b, pos_embed, out_0, out_1):
         def dummy(n):
             for k in range(n):
                 nc.tensor.matmul(junk[:, 0:P], lhsT=wz[:], rhs=wz[:], start=True, stop=True)
-
-        def keep_warm(s, bi, nh):
-            jt = tps.tile([P, 2, 2, P], F32, name="jt", tag="tp")
-            nc.tensor.matmul(
-                jt[:, 0, 0, :], lhsT=wz[:], rhs=o32[(s, bi)][:, NH * nh : NH * nh + P], start=True, stop=True
-            )
 
         make_identity(nc, ident[:])
         nc.gpsimd.memset(prow[:].bitcast(F32), 0.0)
@@ -227,76 +223,72 @@ def tile_tubeletembedding_kernel(tc, video, W, b, pos_embed, out_0, out_1):
         x_rest(0, 0, "S")
         w_copy(0, 1, "S")
         x_T(0, 1)
-        dummy(1)
         x_T(0, 2)
+        dummy(2)
         make_posb(0, 0)
         x_copy(0, 1, 0, 22, "V")
         x_copy(0, 2, 0, 22, "S")
         w_quant(0)
         a_quant(0, 0)
         a_quant(0, 1)
-        dummy(1)
         x_copy(0, 1, 22, 48, "S")
         x_copy(0, 2, 22, 48, "S")
         x_rest(0, 1, "S")
         x_rest(0, 2, "S")
         make_posb(1, 0)
+        x_relay(1, 0, "S")
+        x_relay(1, 1, "S")
 
         banks = [(0, 0, 0), (0, 1, 0), (1, 0, 0), (1, 1, 0), (0, 0, 1), (0, 1, 1), (1, 0, 1), (1, 1, 1)]
         banks += [(0, 2, 0), (0, 2, 1), (0, 3, 0), (0, 3, 1), (1, 2, 0), (1, 2, 1), (2, 0, 0), (2, 0, 1)]
         banks += [(1, 3, 0), (1, 3, 1)]
 
-        def mms(lo, hi):
+        def mms(lo, hi, warm=0):
             for k in range(lo, hi):
-                mm(banks[k][0], banks[k][1], banks[k][2])
+                mm(banks[k][0], banks[k][1], banks[k][2], warm if k == lo else 0)
 
         mms(0, 2)
         w_T(1, 0)
         w_T(1, 1)
+        x_T(1, 0)
         w_copy(1, 0, "S")
         w_copy(1, 1, "S")
+        x_relay(1, 2, "S")
         late8 = []
+        on_v = (10, 13, 17)
         for i, (s, bi, nh) in enumerate(banks):
             add(s, bi, nh)
             if i < 8 or i > 15:
                 st32(s, bi, NH * nh, NH * nh + NH)
             elif nh == 1:
                 st32(s, bi, 0, EMBED)
+            if i - 1 in on_v:
+                cast_v(banks[i - 1][0], banks[i - 1][1], banks[i - 1][2])
             if i == 0:
                 a_quant(1, 0)
                 a_quant(1, 1)
                 mms(2, 4)
-            if i in (1, 2):
-                keep_warm(s, bi, nh)
-            if i == 2:
-                x_relay(1, 0, "V")
-            if i == 3:
-                w_quant(1)
-                make_posb(0, 1)
-                mms(4, 7)
-                x_T(1, 0)
-            if i == 4:
-                mms(7, 8)
-                x_relay(1, 1, "V")
                 x_T(1, 1)
+                x_T(1, 2)
+            if i == 2:
+                w_quant(1)
+                mms(4, 5, 2)
+            if i == 3:
+                make_posb(0, 1)
+            if i in (3, 4, 5):
+                mms(2 + i, 3 + i)
             if i == 5:
                 make_posb(1, 1)
-                x_relay(1, 2, "V")
-                x_T(1, 2)
+                a_quant(0, 2)
                 p2_mm(0)
                 p2_mm(1)
-            if i == 7:
-                a_quant(0, 2)
-                mms(8, 10)
-            if i == 8:
+            if i == 6:
                 a_quant(0, 3)
-                mms(10, 11)
-            if i == 9:
+            if i in (6, 7, 8, 9, 10, 11, 12, 13, 14):
+                mms(2 + i, 3 + i)
+            if i == 8:
                 a_quant(1, 2)
-                mms(11, 12)
-            if i in (10, 11, 12, 13, 14):
-                mms(i + 2, i + 3)
-            if i == 10:
+            if i == 9:
                 a_quant(2, 0)
             if i == 11:
                 a_quant(1, 3)
@@ -304,15 +296,11 @@ def tile_tubeletembedding_kernel(tc, video, W, b, pos_embed, out_0, out_1):
                 mms(17, 18)
             if i == 17:
                 cast_v(s, bi, nh)
-            else:
+            elif i not in on_v:
                 cast(s, bi, nh)
+            if i < 3:
+                x_copy(1, i, 0, 48, "S")
             if i == 3:
-                x_copy(1, 0, 0, 48, "S")
-            if i == 4:
-                x_copy(1, 1, 0, 48, "S")
-            if i == 5:
-                x_copy(1, 2, 0, 48, "S")
-            if i == 7:
                 for jp in range(3):
                     x_rest(1, jp, "S")
             if i == 8:

@@ -24,7 +24,7 @@ def tile_tubeletembedding_kernel(tc, video, W, b, pos_embed, out_0, out_1):
     nc = tc.nc
 
     vid = video[:, :, 0, :, :].rearrange("b (d ts) (i y) x -> ts (b d) i (y x)", ts=2, y=16)
-    wv = W.rearrange("(h p e4) k -> h p (e4 k)", p=P, e4=4)
+    wv = W.rearrange("(g p e) k -> p g (e k)", p=P, e=2)
     pos = pos_embed[0]
     rest0 = out_0[:, 256:288, :].rearrange("b m x -> m b x")
     rest1 = out_1[:, 256:288, :].rearrange("b m x -> m b x")
@@ -41,10 +41,12 @@ def tile_tubeletembedding_kernel(tc, video, W, b, pos_embed, out_0, out_1):
         brow = keep.tile([P, EMBED], BF16, name="brow")
         prow = keep.tile([P, EMBED], BF16, name="prow")
         sel = keep.tile([P, P], BF16, name="sel")
+        bb_sb = keep.tile([P, NH], BF16, name="bb_sb")
+        gate = keep.tile([P, 1], U32, name="gate")
         scr = keep.tile([P, 2], F32, name="scr")
         wz = keep.tile([P, P], F32, name="wz")
         x_raw = [keep.tile([P, 2, 1536], BF16, name="x_raw%d" % h) for h in range(2)]
-        w_raw = [keep.tile([P, 4, 512], BF16, name="w_raw%d" % h) for h in range(2)]
+        w_raw = [keep.tile([P, 2, 1024], BF16, name="w_raw%d" % h) for h in range(2)]
         pos_t = [keep.tile([P, EMBED], BF16, name="pos_t%d" % s) for s in range(2)]
         posb = [keep.tile([P, EMBED], F32, name="posb%d" % s) for s in range(3)]
         y_t = [[keep.tile([P, 2, 2, P], F32, name="y%d_%d" % (h, jp)) for jp in range(3)] for h in range(2)]
@@ -69,23 +71,31 @@ def tile_tubeletembedding_kernel(tc, video, W, b, pos_embed, out_0, out_1):
             else:
                 nc.vector.tensor_copy(out=out, in_=in_)
 
-        def w_T(h, g):
-            ww = w_raw[h][:].bitcast(F32)
-            wt[(h, g)] = tps.tile([P, 2, 2, P], F32, name="wt", tag="tp")
-            for e2 in range(2):
+        def w_T(g):
+            ww = w_raw[g // 2][:, g % 2, :].bitcast(F32).rearrange("p (e w u) -> p e u w", e=2, u=2)
+            wt[g] = tps.tile([P, 2, 2, P], F32, name="wt", tag="tp")
+            for e in range(2):
                 for u in range(2):
-                    nc.tensor.transpose(wt[(h, g)][:, e2, u, :], ww[:, 2 * g + e2, u::2], ident[:])
+                    nc.tensor.transpose(wt[g][:, e, u, :], ww[:, e, u, :], ident[:])
 
-        def w_copy(h, g, eng):
-            dst = w_g[h][:].bitcast(F32).rearrange("k (p e4 u) -> k p e4 u", e4=4, u=2)
-            copy_on(eng, dst[:, :, 2 * g : 2 * g + 2, :], wt[(h, g)][:].rearrange("k e2 u p -> k p e2 u"))
+        def w_copy(g, eng):
+            dst = w_g[g // 2][:].bitcast(F32).rearrange("k (g p e u) -> k g p e u", g=2, e=2, u=2)
+            copy_on(eng, dst[:, g % 2], wt[g][:].rearrange("k e u p -> k p e u"))
 
-        def w_quant(h):
-            nc.vector.quantize_mx(out=w_c[h][:].bitcast(FP8X4), scales=w_s[h][:], in_=w_g[h][:])
+        def w_quant(g, n=1):
+            lo = 256 * (g % 2)
+            nc.vector.quantize_mx(
+                out=w_c[g // 2][:, lo : lo + 256 * n].bitcast(FP8X4),
+                scales=w_s[g // 2][:, lo : lo + 256 * n],
+                in_=w_g[g // 2][:, 4 * lo : 4 * lo + 1024 * n],
+            )
 
         def bb_mm(nh):
             bbp[nh] = bbs.tile([P, NH], F32, name="bbp", tag="bb")
             nc.tensor.matmul(bbp[nh][:], lhsT=ones[:], rhs=brow[:, NH * nh : NH * nh + NH], start=True, stop=True)
+
+        def bb_copy(eng):
+            copy_on(eng, bb_sb[:], bbp[1][:])
 
         def p2_mm(nh):
             bbp[2 + nh] = bbs.tile([P, NH], F32, name="p2p", tag="bb")
@@ -120,23 +130,30 @@ def tile_tubeletembedding_kernel(tc, video, W, b, pos_embed, out_0, out_1):
             src = xt[(h, jp)][:, :, :, 0:96].rearrange("p jj u (b st) -> p b st jj u", b=2)
             copy_on(eng, dst[:, 2 * h : 2 * h + 2, (jp + 1) % 3 : 16 : 3], src[:, :, 48 - n : 48])
 
-        def make_posb(s, nh):
+        def make_posb(s, nh, eng="V"):
             sl = slice(NH * nh, NH * nh + NH)
-            nc.vector.tensor_tensor(out=posb[s][:, sl], in0=pos_t[s][:, sl], in1=bbp[nh][:], op=ALU.add)
+            if eng == "V":
+                nc.vector.tensor_tensor(out=posb[s][:, sl], in0=pos_t[s][:, sl], in1=bbp[nh][:], op=ALU.add)
+            else:
+                nc.gpsimd.tensor_tensor(out=posb[s][:, sl], in0=pos_t[s][:, sl], in1=bb_sb[:], op=ALU.add)
 
-        def a_quant(s, bi):
+        def a_quant(s, bi, n=1):
             h, k = (2, 0) if s == 2 else (bi // 2, ROOM * (bi % 2) + P * s)
             nc.vector.quantize_mx(
-                out=a_c[h][:, k : k + P].bitcast(FP8X4),
-                scales=a_s[h][:, k : k + P],
-                in_=a_g[h][:, 4 * k : 4 * k + 4 * P],
+                out=a_c[h][:, k : k + P * n].bitcast(FP8X4),
+                scales=a_s[h][:, k : k + P * n],
+                in_=a_g[h][:, 4 * k : 4 * k + 4 * P * n],
             )
 
-        def mm(s, bi, nh, warm=0):
-            h, k = (2, 0) if s == 2 else (bi // 2, ROOM * (bi % 2) + P * s)
+        def bank(s, bi, nh, warm=0):
             acc[(s, bi, nh)] = accs.tile([P, NH], F32, name="acc", tag="acc")
             for d in range(warm):
                 nc.tensor.matmul(acc[(s, bi, nh)][:, 0:P], lhsT=wz[:], rhs=wz[:], start=True, stop=True)
+
+        def mm(s, bi, nh):
+            h, k = (2, 0) if s == 2 else (bi // 2, ROOM * (bi % 2) + P * s)
+            if (s, bi, nh) not in acc:
+                bank(s, bi, nh)
             nc.tensor.matmul_mx(
                 out=acc[(s, bi, nh)][:],
                 lhsT=a_c[h][:, k : k + P].bitcast(FP8X4),
@@ -196,14 +213,14 @@ def tile_tubeletembedding_kernel(tc, video, W, b, pos_embed, out_0, out_1):
         brw = b.rearrange("(o e) -> o e", o=1)
         nc.scalar.activation(out=scr[:, 1:2], in_=scr[:, 0:1], func=ACT.Copy, scale=1.0)
 
-        nc.sync.dma_start(out=w_raw[0][:, 0:2, :].rearrange("p e k -> p (e k)"), in_=wv[0, :, 0:1024])
+        nc.sync.dma_start(out=w_raw[0][:, 0, :], in_=wv[:, 0, :])
         for ts in range(2):
             nc.sync.dma_start(out=x_raw[0][0:96, ts, :], in_=vid[ts, 0:16])
         nc.sync.dma_start(out=brow[0:1, :], in_=brw)
-        nc.sync.dma_start(out=w_raw[0][:, 2:4, :].rearrange("p e k -> p (e k)"), in_=wv[0, :, 1024:2048])
+        nc.sync.dma_start(out=w_raw[0][:, 1, :], in_=wv[:, 1, :])
         nc.sync.dma_start(out=pos_t[0][:], in_=pos[0:128, :])
         nc.sync.dma_start(out=pos_t[1][:], in_=pos[128:256, :])
-        nc.sync.dma_start(out=w_raw[1][:].rearrange("p e k -> p (e k)"), in_=wv[1])
+        nc.sync.dma_start(out=w_raw[1][:], in_=wv[:, 2:4, :])
         for ts in range(2):
             nc.sync.dma_start(out=x_raw[1][0:96, ts, :], in_=vid[ts, 16:32])
         nc.sync.dma_start(out=prow[0:32, :], in_=pos[256:288, :])
@@ -211,48 +228,48 @@ def tile_tubeletembedding_kernel(tc, video, W, b, pos_embed, out_0, out_1):
 
         junk = accs.tile([P, NH], F32, name="junk", tag="acc")
         dummy(4)
-        w_T(0, 0)
+        w_T(0)
+        dummy(1)
         bb_mm(0)
-        bb_mm(1)
+        w_copy(0, "S")
         for jp in range(3):
             x_relay(0, jp, "V")
-        w_copy(0, 0, "S")
         x_T(0, 0)
-        w_T(0, 1)
-        x_copy(0, 0, 0, 48, "S")
-        x_rest(0, 0, "S")
-        w_copy(0, 1, "S")
+        w_T(1)
         x_T(0, 1)
         x_T(0, 2)
-        dummy(2)
+        bb_mm(1)
+        dummy(1)
+        w_quant(0)
+        x_copy(0, 0, 0, 22, "S")
         make_posb(0, 0)
+        w_copy(1, "S")
         x_copy(0, 1, 0, 22, "V")
         x_copy(0, 2, 0, 22, "S")
-        w_quant(0)
+        w_quant(1)
         a_quant(0, 0)
         a_quant(0, 1)
-        x_copy(0, 1, 22, 48, "S")
-        x_copy(0, 2, 22, 48, "S")
-        x_rest(0, 1, "S")
-        x_rest(0, 2, "S")
         make_posb(1, 0)
-        x_relay(1, 0, "S")
-        x_relay(1, 1, "S")
+        for jp in range(3):
+            x_copy(0, jp, 22, 48, "S")
+        bb_copy("S")
+        for jp in range(3):
+            x_rest(0, jp, "S")
 
         banks = [(0, 0, 0), (0, 1, 0), (1, 0, 0), (1, 1, 0), (0, 0, 1), (0, 1, 1), (1, 0, 1), (1, 1, 1)]
-        banks += [(0, 2, 0), (0, 2, 1), (0, 3, 0), (0, 3, 1), (1, 2, 0), (1, 2, 1), (2, 0, 0), (2, 0, 1)]
+        banks += [(0, 2, 0), (0, 2, 1), (1, 2, 0), (1, 2, 1), (0, 3, 0), (0, 3, 1), (2, 0, 0), (2, 0, 1)]
         banks += [(1, 3, 0), (1, 3, 1)]
 
-        def mms(lo, hi, warm=0):
+        def mms(lo, hi):
             for k in range(lo, hi):
-                mm(banks[k][0], banks[k][1], banks[k][2], warm if k == lo else 0)
+                mm(banks[k][0], banks[k][1], banks[k][2])
 
         mms(0, 2)
-        w_T(1, 0)
-        w_T(1, 1)
-        x_T(1, 0)
-        w_copy(1, 0, "S")
-        w_copy(1, 1, "S")
+        w_T(2)
+        w_T(3)
+        w_copy(2, "S")
+        w_copy(3, "S")
+        x_relay(1, 0, "S")
         x_relay(1, 2, "S")
         late8 = []
         on_v = (10, 13, 17)
@@ -267,40 +284,35 @@ def tile_tubeletembedding_kernel(tc, video, W, b, pos_embed, out_0, out_1):
             if i == 0:
                 a_quant(1, 0)
                 a_quant(1, 1)
+                nc.gpsimd.tensor_copy(out=gate[:], in_=a_c[0][:, ROOM + P : ROOM + P + 1])
+                make_posb(0, 1, "G")
+                make_posb(1, 1, "G")
                 mms(2, 4)
-                x_T(1, 1)
-                x_T(1, 2)
+            if i == 1:
+                x_relay(1, 1, "V")
+                bank(0, 0, 1, 2)
+                for jp in (1, 0, 2):
+                    x_T(1, jp)
+                    x_copy(1, jp, 0, 48, "S")
+                cast(0, 0, 0)
             if i == 2:
-                w_quant(1)
-                mms(4, 5, 2)
-            if i == 3:
-                make_posb(0, 1)
-            if i in (3, 4, 5):
-                mms(2 + i, 3 + i)
+                w_quant(2, 2)
+                mms(4, 6)
             if i == 5:
-                make_posb(1, 1)
-                a_quant(0, 2)
+                a_quant(0, 2, 2)
                 p2_mm(0)
                 p2_mm(1)
-            if i == 6:
-                a_quant(0, 3)
-            if i in (6, 7, 8, 9, 10, 11, 12, 13, 14):
-                mms(2 + i, 3 + i)
-            if i == 8:
-                a_quant(1, 2)
-            if i == 9:
+            if i == 7:
+                a_quant(0, 3, 2)
+            if i in (3, 4, 5, 6, 7, 8, 9, 10, 11, 12, 13, 14):
+                mms(3 + i, 4 + i)
+            if i == 10:
                 a_quant(2, 0)
-            if i == 11:
-                a_quant(1, 3)
-            if i == 15:
-                mms(17, 18)
             if i == 17:
                 cast_v(s, bi, nh)
-            elif i not in on_v:
+            elif i > 0 and i not in on_v:
                 cast(s, bi, nh)
-            if i < 3:
-                x_copy(1, i, 0, 48, "S")
-            if i == 3:
+            if i == 5:
                 for jp in range(3):
                     x_rest(1, jp, "S")
             if i == 8:

@@ -32,9 +32,9 @@ def tile_tubeletembedding_kernel(tc, video, W, b, pos_embed, out_0, out_1):
     with ExitStack() as ctx:
         keep = ctx.enter_context(tc.tile_pool(name="keep", bufs=1))
         outp = ctx.enter_context(tc.tile_pool(name="outp", bufs=9))
-        tps = ctx.enter_context(tc.psum_pool(name="tps", bufs=3))
+        tps = ctx.enter_context(tc.psum_pool(name="tps", bufs=4))
         accs = ctx.enter_context(tc.psum_pool(name="accs", bufs=3))
-        bbs = ctx.enter_context(tc.psum_pool(name="bbs", bufs=2))
+        bbs = ctx.enter_context(tc.psum_pool(name="bbs", bufs=1))
 
         ident = keep.tile([P, P], F32, name="ident")
         ones = keep.tile([P, P], BF16, name="ones")
@@ -98,7 +98,7 @@ def tile_tubeletembedding_kernel(tc, video, W, b, pos_embed, out_0, out_1):
             copy_on(eng, bb_sb[:], bbp[1][:])
 
         def p2_mm(nh):
-            bbp[2 + nh] = bbs.tile([P, NH], F32, name="p2p", tag="bb")
+            bbp[2 + nh] = tps.tile([P, NH], F32, name="p2p", tag="tp")
             nc.tensor.matmul(bbp[2 + nh][:], lhsT=sel[:], rhs=prow[:, NH * nh : NH * nh + NH], start=True, stop=True)
 
         def p2_copy(nh, eng):
@@ -213,14 +213,13 @@ def tile_tubeletembedding_kernel(tc, video, W, b, pos_embed, out_0, out_1):
         brw = b.rearrange("(o e) -> o e", o=1)
         nc.scalar.activation(out=scr[:, 1:2], in_=scr[:, 0:1], func=ACT.Copy, scale=1.0)
 
-        nc.sync.dma_start(out=w_raw[0][:, 0, :], in_=wv[:, 0, :])
+        nc.sync.dma_start(out=w_raw[0][:], in_=wv[:, 0:2, :])
         for ts in range(2):
             nc.sync.dma_start(out=x_raw[0][0:96, ts, :], in_=vid[ts, 0:16])
         nc.sync.dma_start(out=brow[0:1, :], in_=brw)
-        nc.sync.dma_start(out=w_raw[0][:, 1, :], in_=wv[:, 1, :])
         nc.sync.dma_start(out=pos_t[0][:], in_=pos[0:128, :])
-        nc.sync.dma_start(out=pos_t[1][:], in_=pos[128:256, :])
         nc.sync.dma_start(out=w_raw[1][:], in_=wv[:, 2:4, :])
+        nc.sync.dma_start(out=pos_t[1][:], in_=pos[128:256, :])
         for ts in range(2):
             nc.sync.dma_start(out=x_raw[1][0:96, ts, :], in_=vid[ts, 16:32])
         nc.sync.dma_start(out=prow[0:32, :], in_=pos[256:288, :])
@@ -229,34 +228,37 @@ def tile_tubeletembedding_kernel(tc, video, W, b, pos_embed, out_0, out_1):
         junk = accs.tile([P, NH], F32, name="junk", tag="acc")
         dummy(4)
         w_T(0)
-        dummy(1)
-        bb_mm(0)
+        w_T(1)
         w_copy(0, "S")
+        w_copy(1, "S")
+        dummy(2)
+        bb_mm(0)
         for jp in range(3):
             x_relay(0, jp, "V")
-        x_T(0, 0)
-        w_T(1)
-        x_T(0, 1)
-        x_T(0, 2)
-        bb_mm(1)
-        dummy(1)
-        w_quant(0)
-        x_copy(0, 0, 0, 22, "S")
+        for jp in range(3):
+            x_T(0, jp)
+        w_quant(0, 2)
         make_posb(0, 0)
-        w_copy(1, "S")
-        x_copy(0, 1, 0, 22, "V")
+        x_copy(0, 0, 0, 48, "S")
+        x_rest(0, 0, "S")
+        x_copy(0, 1, 0, 22, "S")
         x_copy(0, 2, 0, 22, "S")
-        w_quant(1)
+        w_T(2)
+        w_T(3)
+        dummy(2)
         a_quant(0, 0)
         a_quant(0, 1)
         make_posb(1, 0)
+        w_copy(2, "S")
+        w_copy(3, "S")
+        x_copy(0, 1, 22, 48, "S")
+        x_copy(0, 2, 22, 48, "S")
+        x_rest(0, 1, "S")
+        x_rest(0, 2, "S")
         for jp in range(3):
-            x_copy(0, jp, 22, 48, "S")
-        bb_copy("S")
-        for jp in range(3):
-            x_rest(0, jp, "S")
+            x_relay(1, jp, "S")
 
-        banks = [(0, 0, 0), (0, 1, 0), (1, 0, 0), (1, 1, 0), (0, 0, 1), (0, 1, 1), (1, 0, 1), (1, 1, 1)]
+        banks = [(0, 0, 0), (0, 1, 0), (0, 0, 1), (0, 1, 1), (1, 0, 0), (1, 0, 1), (1, 1, 0), (1, 1, 1)]
         banks += [(0, 2, 0), (0, 2, 1), (1, 2, 0), (1, 2, 1), (0, 3, 0), (0, 3, 1), (2, 0, 0), (2, 0, 1)]
         banks += [(1, 3, 0), (1, 3, 1)]
 
@@ -265,62 +267,58 @@ def tile_tubeletembedding_kernel(tc, video, W, b, pos_embed, out_0, out_1):
                 mm(banks[k][0], banks[k][1], banks[k][2])
 
         mms(0, 2)
-        w_T(2)
-        w_T(3)
-        w_copy(2, "S")
-        w_copy(3, "S")
-        x_relay(1, 0, "S")
-        x_relay(1, 2, "S")
+        bb_mm(1)
         late8 = []
-        on_v = (10, 13, 17)
+        on_v = (13, 17)
         for i, (s, bi, nh) in enumerate(banks):
             add(s, bi, nh)
-            if i < 8 or i > 15:
-                st32(s, bi, NH * nh, NH * nh + NH)
-            elif nh == 1:
-                st32(s, bi, 0, EMBED)
+            st32(s, bi, NH * nh, NH * nh + NH)
             if i - 1 in on_v:
                 cast_v(banks[i - 1][0], banks[i - 1][1], banks[i - 1][2])
             if i == 0:
-                a_quant(1, 0)
-                a_quant(1, 1)
-                nc.gpsimd.tensor_copy(out=gate[:], in_=a_c[0][:, ROOM + P : ROOM + P + 1])
-                make_posb(0, 1, "G")
-                make_posb(1, 1, "G")
-                mms(2, 4)
-            if i == 1:
-                x_relay(1, 1, "V")
-                bank(0, 0, 1, 2)
-                for jp in (1, 0, 2):
-                    x_T(1, jp)
-                    x_copy(1, jp, 0, 48, "S")
-                cast(0, 0, 0)
-            if i == 2:
                 w_quant(2, 2)
-                mms(4, 6)
+                bank(0, 0, 1, 1)
+                mms(2, 4)
+                x_T(1, 0)
+                x_T(1, 1)
+            if i == 1:
+                make_posb(0, 1)
+                a_quant(1, 0)
+            if i == 2:
+                a_quant(1, 1)
+                mms(4, 5)
+                x_T(1, 2)
+            if i == 4:
+                make_posb(1, 1)
+            if i in (3, 4, 5, 6, 7, 8, 9, 10, 11, 12, 13, 14):
+                mms(2 + i, 3 + i)
             if i == 5:
                 a_quant(0, 2, 2)
+            if i == 6:
+                a_quant(0, 3, 2)
+            if i == 8:
                 p2_mm(0)
                 p2_mm(1)
-            if i == 7:
-                a_quant(0, 3, 2)
-            if i in (3, 4, 5, 6, 7, 8, 9, 10, 11, 12, 13, 14):
-                mms(3 + i, 4 + i)
             if i == 10:
                 a_quant(2, 0)
+            if i == 15:
+                mms(17, 18)
             if i == 17:
                 cast_v(s, bi, nh)
-            elif i > 0 and i not in on_v:
+            elif i not in on_v:
                 cast(s, bi, nh)
-            if i == 5:
+            if i == 2:
+                for jp in range(3):
+                    x_copy(1, jp, 0, 48, "S")
+            if i == 6:
                 for jp in range(3):
                     x_rest(1, jp, "S")
-            if i == 8:
+            if i == 9:
                 p2_copy(0, "S")
-            if i == 10:
+            if i == 11:
                 p2_copy(1, "S")
             if nh == 1:
-                late8.append((i + 2, s, bi))
+                late8.append((i + 1, s, bi))
             while late8 and (late8[0][0] <= i or i == 17):
                 st8(late8[0][1], late8[0][2])
                 late8.pop(0)

@@ -272,7 +272,10 @@ def tile_tubeletembedding_kernel(tc, video, W, b, pos_embed, out_0, out_1):
         on_v = (13, 17)
         for i, (s, bi, nh) in enumerate(banks):
             add(s, bi, nh)
-            st32(s, bi, NH * nh, NH * nh + NH)
+            if i < 8 or i > 15:
+                st32(s, bi, NH * nh, NH * nh + NH)
+            elif nh == 1:
+                st32(s, bi, 0, EMBED)
             if i - 1 in on_v:
                 cast_v(banks[i - 1][0], banks[i - 1][1], banks[i - 1][2])
             if i == 0:
@@ -318,7 +321,7 @@ def tile_tubeletembedding_kernel(tc, video, W, b, pos_embed, out_0, out_1):
             if i == 11:
                 p2_copy(1, "S")
             if nh == 1:
-                late8.append((i + 1, s, bi))
+                late8.append((i + 2, s, bi))
             while late8 and (late8[0][0] <= i or i == 17):
                 st8(late8[0][1], late8[0][2])
                 late8.pop(0)

@@ -217,8 +217,8 @@ def tile_tubeletembedding_kernel(tc, video, W, b, pos_embed, out_0, out_1):
         for ts in range(2):
             nc.sync.dma_start(out=x_raw[0][0:96, ts, :], in_=vid[ts, 0:16])
         nc.sync.dma_start(out=brow[0:1, :], in_=brw)
-        nc.sync.dma_start(out=pos_t[0][:], in_=pos[0:128, :])
         nc.sync.dma_start(out=w_raw[1][:], in_=wv[:, 2:4, :])
+        nc.sync.dma_start(out=pos_t[0][:], in_=pos[0:128, :])
         nc.sync.dma_start(out=pos_t[1][:], in_=pos[128:256, :])
         for ts in range(2):
             nc.sync.dma_start(out=x_raw[1][0:96, ts, :], in_=vid[ts, 16:32])
@@ -231,7 +231,7 @@ def tile_tubeletembedding_kernel(tc, video, W, b, pos_embed, out_0, out_1):
         w_T(1)
         w_copy(0, "S")
         w_copy(1, "S")
-        dummy(2)
+        dummy(3)
         bb_mm(0)
         for jp in range(3):
             x_relay(0, jp, "V")
@@ -245,7 +245,6 @@ def tile_tubeletembedding_kernel(tc, video, W, b, pos_embed, out_0, out_1):
         x_copy(0, 2, 0, 22, "S")
         w_T(2)
         w_T(3)
-        dummy(2)
         a_quant(0, 0)
         a_quant(0, 1)
         make_posb(1, 0)

from contextlib import ExitStack

import concourse.mybir as mybir
from concourse.masks import make_identity

F32 = mybir.dt.float32
BF16 = mybir.dt.bfloat16
U32 = mybir.dt.uint32
U8 = mybir.dt.uint8
FP8X4 = mybir.dt.float8_e4m3fn_x4
FP8 = mybir.dt.float8_e4m3fn
ACT = mybir.ActivationFunctionType
ALU = mybir.AluOpType

P = 128
EMBED = 1024
NH = 512
ROOM = 320
Y_SCALE = 170.0
FLOPS = 2 * 1152 * 512 * 1024


def tile_tubeletembedding_kernel(tc, video, W, b, pos_embed, out_0, out_1):
    nc = tc.nc

    vid = video[:, :, 0, :, :].rearrange("b (d ts) (i y) x -> ts (b d) i (y x)", ts=2, y=16)
    wv = W.rearrange("(g p e) k -> p g (e k)", p=P, e=2)
    pos = pos_embed[0]
    rest0 = out_0[:, 256:288, :].rearrange("b m x -> m b x")
    rest1 = out_1[:, 256:288, :].rearrange("b m x -> m b x")

    with ExitStack() as ctx:
        keep = ctx.enter_context(tc.tile_pool(name="keep", bufs=1))
        outp = ctx.enter_context(tc.tile_pool(name="outp", bufs=9))
        tps = ctx.enter_context(tc.psum_pool(name="tps", bufs=4))
        accs = ctx.enter_context(tc.psum_pool(name="accs", bufs=3))
        bbs = ctx.enter_context(tc.psum_pool(name="bbs", bufs=1))

        ident = keep.tile([P, P], F32, name="ident")
        ones = keep.tile([P, P], BF16, name="ones")
        brow = keep.tile([P, EMBED], BF16, name="brow")
        prow = keep.tile([P, EMBED], BF16, name="prow")
        sel = keep.tile([P, P], BF16, name="sel")
        bb_sb = keep.tile([P, NH], BF16, name="bb_sb")
        gate = keep.tile([P, 1], U32, name="gate")
        scr = keep.tile([P, 2], F32, name="scr")
        wz = keep.tile([P, P], F32, name="wz")
        x_raw = [keep.tile([P, 2, 1536], BF16, name="x_raw%d" % h) for h in range(2)]
        w_raw = [keep.tile([P, 2, 1024], BF16, name="w_raw%d" % h) for h in range(2)]
        pos_t = [keep.tile([P, EMBED], BF16, name="pos_t%d" % s) for s in range(2)]
        posb = [keep.tile([P, EMBED], F32, name="posb%d" % s) for s in range(3)]
        y_t = [[keep.tile([P, 2, 2, P], F32, name="y%d_%d" % (h, jp)) for jp in range(3)] for h in range(2)]
        w_g = [keep.tile([P, 4 * NH], BF16, name="w_g%d" % h, align_bytes=64) for h in range(2)]
        w_c = [keep.tile([P, NH], U32, name="w_c%d" % h, align_bytes=64) for h in range(2)]
        w_s = [keep.tile([P, NH], U8, name="w_s%d" % h, align_bytes=64) for h in range(2)]
        a_cols = [2 * ROOM, 2 * ROOM, P]
        a_g = [keep.tile([P, 4 * a_cols[h]], BF16, name="a_g%d" % h, align_bytes=64) for h in range(3)]
        a_c = [keep.tile([P, a_cols[h]], U32, name="a_c%d" % h, align_bytes=64) for h in range(3)]
        a_s = [keep.tile([P, a_cols[h]], U8, name="a_s%d" % h, align_bytes=64) for h in range(3)]

        wt = {}
        xt = {}
        bbp = {}
        acc = {}
        o32 = {}
        o8 = {}

        def copy_on(eng, out, in_):
            if eng == "S":
                nc.scalar.copy(out=out, in_=in_)
            else:
                nc.vector.tensor_copy(out=out, in_=in_)

        def w_T(g):
            ww = w_raw[g // 2][:, g % 2, :].bitcast(F32).rearrange("p (e w u) -> p e u w", e=2, u=2)
            wt[g] = tps.tile([P, 2, 2, P], F32, name="wt", tag="tp")
            for e in range(2):
                for u in range(2):
                    nc.tensor.transpose(wt[g][:, e, u, :], ww[:, e, u, :], ident[:])

        def w_copy(g, eng):
            dst = w_g[g // 2][:].bitcast(F32).rearrange("k (g p e u) -> k g p e u", g=2, e=2, u=2)
            copy_on(eng, dst[:, g % 2], wt[g][:].rearrange("k e u p -> k p e u"))

        def w_quant(g, n=1):
            lo = 256 * (g % 2)
            nc.vector.quantize_mx(
                out=w_c[g // 2][:, lo : lo + 256 * n].bitcast(FP8X4),
                scales=w_s[g // 2][:, lo : lo + 256 * n],
                in_=w_g[g // 2][:, 4 * lo : 4 * lo + 1024 * n],
            )

        def bb_mm(nh):
            bbp[nh] = bbs.tile([P, NH], F32, name="bbp", tag="bb")
            nc.tensor.matmul(bbp[nh][:], lhsT=ones[:], rhs=brow[:, NH * nh : NH * nh + NH], start=True, stop=True)

        def bb_copy(eng):
            copy_on(eng, bb_sb[:], bbp[1][:])

        def p2_mm(nh):
            bbp[2 + nh] = tps.tile([P, NH], F32, name="p2p", tag="tp")
            nc.tensor.matmul(bbp[2 + nh][:], lhsT=sel[:], rhs=prow[:, NH * nh : NH * nh + NH], start=True, stop=True)

        def p2_copy(nh, eng):
            copy_on(eng, posb[2][:, NH * nh : NH * nh + NH], bbp[2 + nh][:])

        def x_relay(h, jp, eng):
            xw = x_raw[h][:].bitcast(F32).rearrange("p ts (py j wq u) -> p j u (ts py) wq", py=16, j=6, wq=4, u=2)
            copy_on(
                eng,
                y_t[h][jp][:].rearrange("p jj u (tp wq) -> p jj u tp wq", wq=4),
                xw[:, 2 * jp : 2 * jp + 2],
            )

        def x_T(h, jp):
            xt[(h, jp)] = tps.tile([P, 2, 2, P], F32, name="xt", tag="tp")
            for jj in range(2):
                for u in range(2):
                    nc.tensor.transpose(xt[(h, jp)][:, jj, u, :], y_t[h][jp][:, jj, u, :], ident[:])

        def x_copy(h, jp, lo, hi, eng):
            dst = a_g[h][:].bitcast(F32).rearrange("p (b c) -> p b c", b=2)[:, :, 0:576]
            dst = dst.rearrange("p b (st j3 jj u) -> p b st j3 jj u", j3=3, jj=2, u=2)
            src = xt[(h, jp)][:, :, :, 0:96].rearrange("p jj u (b st) -> p b st jj u", b=2)
            copy_on(eng, dst[:, :, lo:hi, jp], src[:, :, lo:hi])

        def x_rest(h, jp, eng):
            n = 6 if jp == 2 else 5
            dst = a_g[2][:].bitcast(F32).rearrange("p (pr jj b u) -> p b pr jj u", b=4, jj=2, u=2)
            src = xt[(h, jp)][:, :, :, 0:96].rearrange("p jj u (b st) -> p b st jj u", b=2)
            copy_on(eng, dst[:, 2 * h : 2 * h + 2, (jp + 1) % 3 : 16 : 3], src[:, :, 48 - n : 48])

        def make_posb(s, nh, eng="V"):
            sl = slice(NH * nh, NH * nh + NH)
            if eng == "V":
                nc.vector.tensor_tensor(out=posb[s][:, sl], in0=pos_t[s][:, sl], in1=bbp[nh][:], op=ALU.add)
            else:
                nc.gpsimd.tensor_tensor(out=posb[s][:, sl], in0=pos_t[s][:, sl], in1=bb_sb[:], op=ALU.add)

        def a_quant(s, bi, n=1):
            h, k = (2, 0) if s == 2 else (bi // 2, ROOM * (bi % 2) + P * s)
            nc.vector.quantize_mx(
                out=a_c[h][:, k : k + P * n].bitcast(FP8X4),
                scales=a_s[h][:, k : k + P * n],
                in_=a_g[h][:, 4 * k : 4 * k + 4 * P * n],
            )

        def bank(s, bi, nh, warm=0):
            acc[(s, bi, nh)] = accs.tile([P, NH], F32, name="acc", tag="acc")
            for d in range(warm):
                nc.tensor.matmul(acc[(s, bi, nh)][:, 0:P], lhsT=wz[:], rhs=wz[:], start=True, stop=True)

        def mm(s, bi, nh):
            h, k = (2, 0) if s == 2 else (bi // 2, ROOM * (bi % 2) + P * s)
            if (s, bi, nh) not in acc:
                bank(s, bi, nh)
            nc.tensor.matmul_mx(
                out=acc[(s, bi, nh)][:],
                lhsT=a_c[h][:, k : k + P].bitcast(FP8X4),
                lhsT_scale=a_s[h][:, k : k + P],
                rhs=w_c[nh][:].bitcast(FP8X4),
                rhs_scale=w_s[nh][:],
                start=True,
                stop=True,
            )

        def add(s, bi, nh):
            if (s, bi) not in o32:
                o32[(s, bi)] = outp.tile([P, EMBED], F32, name="o32", tag="o32")
                o8[(s, bi)] = outp.tile([P, EMBED], FP8, name="o8", tag="o8")
            sl = slice(NH * nh, NH * nh + NH)
            nc.vector.tensor_tensor(out=o32[(s, bi)][:, sl], in0=acc[(s, bi, nh)][:], in1=posb[s][:, sl], op=ALU.add)

        def cast(s, bi, nh):
            sl = slice(NH * nh, NH * nh + NH)
            nc.scalar.activation(
                out=o8[(s, bi)][:, sl], in_=o32[(s, bi)][:, sl], func=ACT.Copy, scale=Y_SCALE, saturate=False
            )

        def cast_v(s, bi, nh):
            sl = slice(NH * nh, NH * nh + NH)
            nc.vector.tensor_scalar(
                out=o8[(s, bi)][:, sl], in0=o32[(s, bi)][:, sl], scalar1=Y_SCALE, scalar2=None, op0=ALU.mult,
                saturate=False,
            )

        def st32(s, bi, lo, hi):
            d0 = out_0[bi, P * s : P * s + P, lo:hi] if s < 2 else rest0[:, :, lo:hi]
            nc.sync.dma_start(out=d0, in_=o32[(s, bi)][:, lo:hi])

        def st8(s, bi):
            d1 = out_1[bi, P * s : P * s + P, :] if s < 2 else rest1
            nc.sync.dma_start(out=d1, in_=o8[(s, bi)][:].bitcast(U8))

        def dummy(n):
            for k in range(n):
                nc.tensor.matmul(junk[:, 0:P], lhsT=wz[:], rhs=wz[:], start=True, stop=True)

        make_identity(nc, ident[:])
        nc.gpsimd.memset(prow[:].bitcast(F32), 0.0)
        nc.gpsimd.memset(sel[:], 0.0)
        for bi in range(4):
            nc.gpsimd.tensor_copy(out=sel[:, bi::4], in_=ident[:, 0:32])
        nc.gpsimd.memset(sel[32:33, :], 1.0)
        nc.vector.memset(wz[:], 0.0)
        nc.vector.memset(brow[:].bitcast(F32), 0.0)
        nc.vector.memset(ones[:], 1.0)
        nc.vector.memset(scr[:], 0.0)
        nc.vector.memset(x_raw[0][96:128].bitcast(F32), 0.0)
        nc.gpsimd.memset(x_raw[1][96:128].bitcast(F32), 0.0)

        ctx.enter_context(tc.manual_schedule())
        brw = b.rearrange("(o e) -> o e", o=1)
        nc.scalar.activation(out=scr[:, 1:2], in_=scr[:, 0:1], func=ACT.Copy, scale=1.0)

        nc.sync.dma_start(out=w_raw[0][:], in_=wv[:, 0:2, :])
        for ts in range(2):
            nc.sync.dma_start(out=x_raw[0][0:96, ts, :], in_=vid[ts, 0:16])
        nc.sync.dma_start(out=brow[0:1, :], in_=brw)
        nc.sync.dma_start(out=w_raw[1][:], in_=wv[:, 2:4, :])
        nc.sync.dma_start(out=pos_t[0][:], in_=pos[0:128, :])
        nc.sync.dma_start(out=pos_t[1][:], in_=pos[128:256, :])
        for ts in range(2):
            nc.sync.dma_start(out=x_raw[1][0:96, ts, :], in_=vid[ts, 16:32])
        nc.sync.dma_start(out=prow[0:32, :], in_=pos[256:288, :])
        nc.sync.dma_start(out=prow[32:33, :], in_=brw)

        junk = accs.tile([P, NH], F32, name="junk", tag="acc")
        dummy(4)
        w_T(0)
        w_T(1)
        w_copy(0, "S")
        w_copy(1, "S")
        dummy(3)
        bb_mm(0)
        for jp in range(3):
            x_relay(0, jp, "V")
        for jp in range(3):
            x_T(0, jp)
        w_quant(0, 2)
        make_posb(0, 0)
        x_copy(0, 0, 0, 48, "S")
        x_rest(0, 0, "S")
        x_copy(0, 1, 0, 22, "S")
        x_copy(0, 2, 0, 22, "S")
        w_T(2)
        w_T(3)
        a_quant(0, 0)
        a_quant(0, 1)
        make_posb(1, 0)
        w_copy(2, "S")
        w_copy(3, "S")
        x_copy(0, 1, 22, 48, "S")
        x_copy(0, 2, 22, 48, "S")
        x_rest(0, 1, "S")
        x_rest(0, 2, "S")
        for jp in range(3):
            x_relay(1, jp, "S")

        banks = [(0, 0, 0), (0, 1, 0), (0, 0, 1), (0, 1, 1), (1, 0, 0), (1, 0, 1), (1, 1, 0), (1, 1, 1)]
        banks += [(0, 2, 0), (0, 2, 1), (1, 2, 0), (1, 2, 1), (0, 3, 0), (0, 3, 1), (2, 0, 0), (2, 0, 1)]
        banks += [(1, 3, 0), (1, 3, 1)]

        def mms(lo, hi):
            for k in range(lo, hi):
                mm(banks[k][0], banks[k][1], banks[k][2])

        mms(0, 2)
        bb_mm(1)
        late8 = []
        on_v = (13, 17)
        for i, (s, bi, nh) in enumerate(banks):
            add(s, bi, nh)
            if i < 8 or i > 15:
                st32(s, bi, NH * nh, NH * nh + NH)
            elif nh == 1:
                st32(s, bi, 0, EMBED)
            if i - 1 in on_v:
                cast_v(banks[i - 1][0], banks[i - 1][1], banks[i - 1][2])
            if i == 0:
                w_quant(2, 2)
                bank(0, 0, 1, 1)
                mms(2, 4)
                x_T(1, 0)
                x_T(1, 1)
            if i == 1:
                make_posb(0, 1)
                a_quant(1, 0)
            if i == 2:
                a_quant(1, 1)
                mms(4, 5)
                x_T(1, 2)
            if i == 4:
                make_posb(1, 1)
            if i in (3, 4, 5, 6, 7, 8, 9, 10, 11, 12, 13, 14):
                mms(2 + i, 3 + i)
            if i == 5:
                a_quant(0, 2, 2)
            if i == 6:
                a_quant(0, 3, 2)
            if i == 8:
                p2_mm(0)
                p2_mm(1)
            if i == 10:
                a_quant(2, 0)
            if i == 15:
                mms(17, 18)
            if i == 17:
                cast_v(s, bi, nh)
            elif i not in on_v:
                cast(s, bi, nh)
            if i == 2:
                for jp in range(3):
                    x_copy(1, jp, 0, 48, "S")
            if i == 6:
                for jp in range(3):
                    x_rest(1, jp, "S")
            if i == 9:
                p2_copy(0, "S")
            if i == 11:
                p2_copy(1, "S")
            if nh == 1:
                late8.append((i + 2, s, bi))
            while late8 and (late8[0][0] <= i or i == 17):
                st8(late8[0][1], late8[0][2])
                late8.pop(0)
